import numpy as np
import ml_dtypes


def mxq(x, axis, fmt="e4m3"):
    dtype, down = {"e4m3": (ml_dtypes.float8_e4m3fn, 7), "e5m2": (ml_dtypes.float8_e5m2, 14)}[fmt]
    v = np.moveaxis(np.asarray(x, np.float32).astype(ml_dtypes.bfloat16).astype(np.float64), axis, -1)
    blocks = v.reshape(v.shape[:-1] + (-1, 32))
    amax = np.abs(blocks).max(-1, keepdims=True)
    byte = np.maximum(np.where(amax > 0, np.frexp(amax)[1] - 1 + 127, 0) - down, 1)
    scale = np.exp2(byte - 127.0)
    codes = (blocks / scale).astype(np.float32).astype(dtype).astype(np.float64)
    return np.moveaxis((codes * scale).reshape(v.shape), -1, axis)


WIDE = False


def mx_kscale(k):
    if not WIDE:
        return np.ones(k)
    levels = np.array([10, -10, 5, -5, 0])
    a = np.random.permutation(np.resize(levels, k // 512 * 4)).reshape(k // 512, 4)
    idx = np.arange(k)
    return np.exp2(a[idx // 512, idx % 128 // 32])


BF16 = ml_dtypes.bfloat16


def bf(x):
    return np.asarray(x, np.float32).astype(BF16)


def f64(x):
    return np.asarray(x).astype(np.float64)


N, T, H, P0, P1, C0, NC, V0, V1 = 2, 256, 2048, 512, 128, 20000, 2, 8192, 12288


def setup_inputs():
    s, t = mx_kscale(H), mx_kscale(P0)
    return {"x": bf(np.random.standard_normal((N, T, H)) * s),
            "tail_proj_0": bf(np.random.standard_normal((H, P0)) / np.sqrt(H) / s[:, None] * t),
            "tail_w_0": bf(np.random.standard_normal((P0, V0)) * 2.0 / np.sqrt(P0) / t[:, None]),
            "cluster_prob": bf(0.05 + 0.55 * np.random.random((N, T))[..., None])}


def reference(x, tail_proj_0, tail_w_0, cluster_prob):
    h = mxq(f64(x), 2, "e4m3") @ mxq(f64(tail_proj_0), 0, "e4m3")
    logits = mxq(h, 2, "e4m3") @ mxq(f64(tail_w_0), 0, "e4m3")
    e = np.exp(logits - logits.max(-1, keepdims=True))
    return e / e.sum(-1, keepdims=True) * f64(cluster_prob)

@@ -1,0 +1,226 @@
+from contextlib import ExitStack
+
+import concourse.mybir as mybir
+from concourse.masks import make_identity
+
+F32 = mybir.dt.float32
+BF16 = mybir.dt.bfloat16
+U32 = mybir.dt.uint32
+U8 = mybir.dt.uint8
+FP8X4 = mybir.dt.float8_e4m3fn_x4
+AF = mybir.ActivationFunctionType
+ALU = mybir.AluOpType
+AX = mybir.AxisListType
+
+P = 128
+TOK = 512
+H = 2048
+P0 = 512
+V0 = 8192
+FLOPS = 2 * TOK * H * P0 + 2 * TOK * P0 * V0
+
+RAW_BUFS = 5
+W_CHUNK = 1024
+N_CHUNKS = V0 // W_CHUNK
+GROUP = 2048
+BANK = 512
+W_V_COLS = 512
+PROJ_V_COLS = 256
+
+
+def regroup(copy, dst, src, col0, col1):
+    d = dst.rearrange("p (c i t) -> p c t i", i=4, t=4)[:, col0 // 4:col1 // 4, :, :]
+    s = src.rearrange("p (t c i) -> p c t i", t=4, i=4)[:, col0 // 4:col1 // 4, :, :]
+    copy(out=d, in_=s)
+
+
+def tile_adaptiveinputsoftmax_pa_kernel(tc, x, tail_proj_0, tail_w_0, cluster_prob, out):
+    nc = tc.nc
+    x_rows = x.rearrange("n t h -> (n t) h").rearrange("(i p) k -> p i k", p=P)
+    proj_rows = tail_proj_0.rearrange("(a p e) n -> p a (e n)", p=P, e=2)
+    w_rows = tail_w_0.rearrange("(j p) n -> p j n", p=P)
+    out_rows = out.rearrange("n t v -> (n t) v")
+    prob_cols = cluster_prob.rearrange("n t o -> (n t o)").rearrange("(c p) -> p c", p=P)
+
+    with ExitStack() as ctx:
+        keep = ctx.enter_context(tc.tile_pool(name="keep", bufs=1))
+        raw = ctx.enter_context(tc.tile_pool(name="raw", bufs=RAW_BUFS))
+        grp = ctx.enter_context(tc.tile_pool(name="grp", bufs=3))
+        hgrp = ctx.enter_context(tc.tile_pool(name="hgrp", bufs=2))
+        epool = ctx.enter_context(tc.tile_pool(name="epool", bufs=12))
+        stat = ctx.enter_context(tc.tile_pool(name="stat", bufs=4))
+        gstat = ctx.enter_context(tc.tile_pool(name="gstat", bufs=4))
+        psum = ctx.enter_context(tc.psum_pool(name="psum", bufs=8))
+
+        ident = keep.tile([P, P], F32, name="ident")
+        make_identity(nc, ident[:])
+        warm = keep.tile([P, 1], F32, name="warm")
+        nc.vector.memset(warm[:], 0.0)
+        warm2 = keep.tile([P, 1], F32, name="warm2")
+        nc.scalar.activation(out=warm2[:], in_=warm[:], func=AF.Exp)
+
+        prob_bf = keep.tile([P, 4], BF16, name="prob_bf")
+        with nc.allow_non_contiguous_dma(reason="512 two-byte values, one column per token tile"):
+            nc.scalar.dma_start(out=prob_bf[:], in_=prob_cols)
+        prob = keep.tile([P, 4], F32, name="prob")
+        nc.vector.tensor_copy(out=prob[:], in_=prob_bf[:])
+
+        pq = keep.tile([P, 4 * P0], U32, name="pq", align_bytes=64)
+        ps = keep.tile([P, 4 * P0], U8, name="ps", align_bytes=64)
+        xq = keep.tile([P, 4 * TOK], U32, name="xq", align_bytes=64)
+        xs = keep.tile([P, 4 * TOK], U8, name="xs", align_bytes=64)
+        hq = keep.tile([P, TOK], U32, name="hq", align_bytes=64)
+        hs = keep.tile([P, TOK], U8, name="hs", align_bytes=64)
+        wq = keep.tile([P, V0], U32, name="wq", align_bytes=64)
+        ws = keep.tile([P, V0], U8, name="ws", align_bytes=64)
+
+        loaded = {}
+
+        def load(unit):
+            kind, idx = unit
+            t = raw.tile([P, 4096], BF16, name="rawt", tag="raw")
+            if kind == "proj":
+                nc.sync.dma_start(out=t[:].rearrange("p (a f) -> p a f", a=4), in_=proj_rows[:, 4 * idx:4 * idx + 4, :])
+            elif kind == "x":
+                nc.sync.dma_start(out=t[:].rearrange("p (i k) -> p i k", i=2), in_=x_rows[:, 2 * idx:2 * idx + 2, :])
+            else:
+                nc.sync.dma_start(out=t[:].rearrange("p (j n) -> p j n", j=4), in_=w_rows[:, :, W_CHUNK * idx:W_CHUNK * (idx + 1)])
+            loaded[unit] = t
+
+        def prep_proj(idx):
+            t = loaded[("proj", idx)]
+            g = grp.tile([P, 4096], BF16, name="grpt", tag="grp", align_bytes=64)
+            for gl in range(2):
+                sl = slice(2048 * gl, 2048 * (gl + 1))
+                regroup(nc.vector.tensor_copy, g[:, sl], t[:, sl], 0, PROJ_V_COLS)
+                regroup(nc.scalar.copy, g[:, sl], t[:, sl], PROJ_V_COLS, P0)
+            cols = slice(1024 * idx, 1024 * (idx + 1))
+            nc.vector.quantize_mx(out=pq[:, cols].bitcast(FP8X4), scales=ps[:, cols], in_=g[:])
+
+        def prep_x(idx):
+            t = loaded[("x", idx)]
+            words = t[:].bitcast(F32)
+            g = grp.tile([P, 4096], BF16, name="grpt", tag="grp", align_bytes=64)
+            gwords = g[:].bitcast(F32)
+            banks = []
+            for gp in range(4):
+                bank = psum.tile([P, BANK], F32, name="bank", tag="ps")
+                for u in range(2):
+                    for i in range(2):
+                        src0 = 1024 * i + 256 * gp + 128 * u
+                        nc.tensor.transpose(out=bank[:, 256 * u + 128 * i:256 * u + 128 * (i + 1)],
+                                            in_=words[:, src0:src0 + 128], identity=ident[:])
+                banks.append(bank)
+            for gp in range(4):
+                nc.scalar.copy(out=gwords[:, 512 * gp:512 * (gp + 1)].rearrange("p (w u) -> p w u", u=2),
+                               in_=banks[gp][:].rearrange("p (u w) -> p w u", u=2))
+            cols = slice(1024 * idx, 1024 * (idx + 1))
+            nc.vector.quantize_mx(out=xq[:, cols].bitcast(FP8X4), scales=xs[:, cols], in_=g[:])
+
+        def hidden(tt):
+            bank = psum.tile([P, BANK], F32, name="bank", tag="ps")
+            for j in range(4):
+                for gp in range(4):
+                    a = slice(512 * gp + 128 * j, 512 * gp + 128 * (j + 1))
+                    b0 = 1024 * (tt // 2) + 256 * gp + 128 * (tt % 2)
+                    b = slice(b0, b0 + 128)
+                    nc.tensor.matmul_mx(out=bank[:, 128 * j:128 * (j + 1)],
+                                        lhsT=pq[:, a].bitcast(FP8X4), lhsT_scale=ps[:, a],
+                                        rhs=xq[:, b].bitcast(FP8X4), rhs_scale=xs[:, b],
+                                        start=(gp == 0), stop=(gp == 3))
+            g = hgrp.tile([P, 512], BF16, name="hg", tag="hg", align_bytes=64)
+            nc.scalar.copy(out=g[:].rearrange("p (w j) -> p w j", j=4),
+                           in_=bank[:].rearrange("p (j w) -> p w j", j=4))
+            cols = slice(128 * tt, 128 * (tt + 1))
+            nc.vector.quantize_mx(out=hq[:, cols].bitcast(FP8X4), scales=hs[:, cols], in_=g[:])
+
+        def prep_w(idx):
+            t = loaded[("w", idx)]
+            g = grp.tile([P, 4096], BF16, name="grpt", tag="grp", align_bytes=64)
+            regroup(nc.vector.tensor_copy, g[:], t[:], 0, W_V_COLS)
+            regroup(nc.scalar.copy, g[:], t[:], W_V_COLS, W_CHUNK)
+            cols = slice(W_CHUNK * idx, W_CHUNK * (idx + 1))
+            nc.vector.quantize_mx(out=wq[:, cols].bitcast(FP8X4), scales=ws[:, cols], in_=g[:])
+
+        state = {}
+
+        def start_tile(tt):
+            state[tt] = {
+                "nm4": stat.tile([P, 4], F32, name="nm4", tag="nm4"),
+                "s16": stat.tile([P, 16], F32, name="s16", tag="s16"),
+                "e": [],
+            }
+
+        def logits_group(tt, g):
+            st = state[tt]
+            tcols = slice(128 * tt, 128 * (tt + 1))
+            gm = gstat.tile([P, 4], F32, name="gm", tag="gm")
+            e = epool.tile([P, GROUP], F32, name="e", tag="e")
+            banks = []
+            for i in range(4):
+                bank = psum.tile([P, BANK], F32, name="bank", tag="ps")
+                n = slice(GROUP * g + BANK * i, GROUP * g + BANK * (i + 1))
+                nc.tensor.matmul_mx(out=bank[:], lhsT=hq[:, tcols].bitcast(FP8X4), lhsT_scale=hs[:, tcols],
+                                    rhs=wq[:, n].bitcast(FP8X4), rhs_scale=ws[:, n], start=True, stop=True)
+                banks.append(bank)
+            for i in range(4):
+                nc.vector.tensor_reduce(out=gm[:, i:i + 1], in_=banks[i][:], axis=AX.X, op=ALU.max)
+            nc.vector.tensor_reduce(out=st["nm4"][:, g:g + 1], in_=gm[:], axis=AX.X, op=ALU.max, negate=True)
+            for i in range(4):
+                nc.scalar.activation(out=e[:, BANK * i:BANK * (i + 1)], in_=banks[i][:], func=AF.Exp,
+                                     bias=st["nm4"][:, g:g + 1], scale=1.0,
+                                     accum_out=st["s16"][:, 4 * g + i:4 * g + i + 1])
+            st["e"].append(e)
+
+        def finish(tt, engines):
+            st = state[tt]
+            nmax = stat.tile([P, 1], F32, name="nmax", tag="nmax")
+            nc.vector.tensor_reduce(out=nmax[:], in_=st["nm4"][:], axis=AX.X, op=ALU.min)
+            f4 = stat.tile([P, 4], F32, name="f4", tag="f4")
+            nc.scalar.activation(out=f4[:], in_=st["nm4"][:], func=AF.Exp, bias=nmax[:], scale=-1.0)
+            s4 = stat.tile([P, 4], F32, name="s4", tag="s4")
+            nc.vector.tensor_reduce(out=s4[:], in_=st["s16"][:].rearrange("p (g i) -> p g i", i=4), axis=AX.X, op=ALU.add)
+            fs = stat.tile([P, 4], F32, name="fs", tag="fs")
+            nc.vector.tensor_tensor(out=fs[:], in0=f4[:], in1=s4[:], op=ALU.mult)
+            tot = stat.tile([P, 1], F32, name="tot", tag="tot")
+            nc.vector.tensor_reduce(out=tot[:], in_=fs[:], axis=AX.X, op=ALU.add)
+            rtot = stat.tile([P, 1], F32, name="rtot", tag="rtot")
+            nc.vector.reciprocal(out=rtot[:], in_=tot[:])
+            sc4 = stat.tile([P, 4], F32, name="sc4", tag="sc4")
+            nc.vector.tensor_scalar(out=sc4[:], in0=f4[:], scalar1=rtot[:], scalar2=prob[:, tt:tt + 1],
+                                    op0=ALU.mult, op1=ALU.mult)
+            for g in range(4):
+                e = st["e"][g]
+                s = sc4[:, g:g + 1]
+                if engines[g] == "g":
+                    nc.gpsimd.tensor_scalar(out=e[:], in0=e[:], scalar1=s, scalar2=0.0, op0=ALU.mult, op1=ALU.add)
+                elif engines[g] == "v":
+                    nc.vector.tensor_scalar(out=e[:], in0=e[:], scalar1=s, scalar2=None, op0=ALU.mult)
+                else:
+                    nc.scalar.activation(out=e[:], in_=e[:], func=AF.Copy, scale=s)
+                nc.sync.dma_start(out=out_rows[128 * tt:128 * (tt + 1), GROUP * g:GROUP * (g + 1)], in_=e[:])
+
+        units = [("proj", 0), ("proj", 1), ("x", 0), ("x", 1)] + [("w", c) for c in range(N_CHUNKS)]
+        for u in units[:RAW_BUFS]:
+            load(u)
+        start_tile(0)
+        for n, unit in enumerate(units):
+            kind, idx = unit
+            if kind == "proj":
+                prep_proj(idx)
+            elif kind == "x":
+                prep_x(idx)
+                hidden(2 * idx)
+                hidden(2 * idx + 1)
+            else:
+                prep_w(idx)
+                if idx % 2 == 1:
+                    logits_group(0, idx // 2)
+            if n + RAW_BUFS < len(units):
+                load(units[n + RAW_BUFS])
+        finish(0, "gggg")
+        for tt in range(1, 4):
+            start_tile(tt)
+            for g in range(4):
+                logits_group(tt, g)
+            finish(tt, "gggg" if tt < 3 else "vvsg")

@@ -19,13 +19,18 @@ P0 = 512
 V0 = 8192
 FLOPS = 2 * TOK * H * P0 + 2 * TOK * P0 * V0
 
-RAW_BUFS = 5
 W_CHUNK = 1024
 N_CHUNKS = V0 // W_CHUNK
 GROUP = 2048
 BANK = 512
-W_V_COLS = 512
+
+RAW_BUFS = 5
+W_V_COLS = [448] * 8
 PROJ_V_COLS = 256
+X_V_BANKS = 1
+TAIL = [(0, "v", 0, 512), (0, "v", 512, 2048), (3, "s", 0, 2048), (1, "v", 0, 2048), (2, "v", 0, 2048)]
+FIN_LAG = 4
+MID = ["gggg", "gggg", "gggg"]
 
 
 def regroup(copy, dst, src, col0, col1):
@@ -51,6 +56,7 @@ def tile_adaptiveinputsoftmax_pa_kernel(tc, x, tail_proj_0, tail_w_0, cluster_pr
         stat = ctx.enter_context(tc.tile_pool(name="stat", bufs=4))
         gstat = ctx.enter_context(tc.tile_pool(name="gstat", bufs=4))
         psum = ctx.enter_context(tc.psum_pool(name="psum", bufs=8))
+        ctx.enter_context(tc.manual_schedule())
 
         ident = keep.tile([P, P], F32, name="ident")
         make_identity(nc, ident[:])
@@ -58,12 +64,6 @@ def tile_adaptiveinputsoftmax_pa_kernel(tc, x, tail_proj_0, tail_w_0, cluster_pr
         nc.vector.memset(warm[:], 0.0)
         warm2 = keep.tile([P, 1], F32, name="warm2")
         nc.scalar.activation(out=warm2[:], in_=warm[:], func=AF.Exp)
-
-        prob_bf = keep.tile([P, 4], BF16, name="prob_bf")
-        with nc.allow_non_contiguous_dma(reason="512 two-byte values, one column per token tile"):
-            nc.scalar.dma_start(out=prob_bf[:], in_=prob_cols)
-        prob = keep.tile([P, 4], F32, name="prob")
-        nc.vector.tensor_copy(out=prob[:], in_=prob_bf[:])
 
         pq = keep.tile([P, 4 * P0], U32, name="pq", align_bytes=64)
         ps = keep.tile([P, 4 * P0], U8, name="ps", align_bytes=64)
@@ -75,8 +75,14 @@ def tile_adaptiveinputsoftmax_pa_kernel(tc, x, tail_proj_0, tail_w_0, cluster_pr
         ws = keep.tile([P, V0], U8, name="ws", align_bytes=64)
 
         loaded = {}
+        grouped = {}
+        units = [("proj", 0), ("proj", 1), ("x", 0), ("x", 1)] + [("w", c) for c in range(N_CHUNKS)]
+        queue = list(units)
 
-        def load(unit):
+        def load_next():
+            if not queue:
+                return
+            unit = queue.pop(0)
             kind, idx = unit
             t = raw.tile([P, 4096], BF16, name="rawt", tag="raw")
             if kind == "proj":
@@ -87,21 +93,29 @@ def tile_adaptiveinputsoftmax_pa_kernel(tc, x, tail_proj_0, tail_w_0, cluster_pr
                 nc.sync.dma_start(out=t[:].rearrange("p (j n) -> p j n", j=4), in_=w_rows[:, :, W_CHUNK * idx:W_CHUNK * (idx + 1)])
             loaded[unit] = t
 
-        def prep_proj(idx):
-            t = loaded[("proj", idx)]
-            g = grp.tile([P, 4096], BF16, name="grpt", tag="grp", align_bytes=64)
+        def new_grouped(unit):
+            grouped[unit] = grp.tile([P, 4096], BF16, name="grpt", tag="grp", align_bytes=64)
+
+        def proj_regroup(idx):
+            unit = ("proj", idx)
+            new_grouped(unit)
             for gl in range(2):
                 sl = slice(2048 * gl, 2048 * (gl + 1))
-                regroup(nc.vector.tensor_copy, g[:, sl], t[:, sl], 0, PROJ_V_COLS)
-                regroup(nc.scalar.copy, g[:, sl], t[:, sl], PROJ_V_COLS, P0)
-            cols = slice(1024 * idx, 1024 * (idx + 1))
-            nc.vector.quantize_mx(out=pq[:, cols].bitcast(FP8X4), scales=ps[:, cols], in_=g[:])
+                regroup(nc.vector.tensor_copy, grouped[unit][:, sl], loaded[unit][:, sl], 0, PROJ_V_COLS)
+                if PROJ_V_COLS < P0:
+                    regroup(nc.scalar.copy, grouped[unit][:, sl], loaded[unit][:, sl], PROJ_V_COLS, P0)
 
-        def prep_x(idx):
-            t = loaded[("x", idx)]
-            words = t[:].bitcast(F32)
-            g = grp.tile([P, 4096], BF16, name="grpt", tag="grp", align_bytes=64)
-            gwords = g[:].bitcast(F32)
+        def quantise(unit):
+            kind, idx = unit
+            codes, scales = {"proj": (pq, ps), "x": (xq, xs), "w": (wq, ws)}[kind]
+            cols = slice(1024 * idx, 1024 * (idx + 1))
+            nc.vector.quantize_mx(out=codes[:, cols].bitcast(FP8X4), scales=scales[:, cols], in_=grouped[unit][:])
+
+        def x_transpose(idx):
+            unit = ("x", idx)
+            new_grouped(unit)
+            words = loaded[unit][:].bitcast(F32)
+            gwords = grouped[unit][:].bitcast(F32)
             banks = []
             for gp in range(4):
                 bank = psum.tile([P, BANK], F32, name="bank", tag="ps")
@@ -112,12 +126,14 @@ def tile_adaptiveinputsoftmax_pa_kernel(tc, x, tail_proj_0, tail_w_0, cluster_pr
                                             in_=words[:, src0:src0 + 128], identity=ident[:])
                 banks.append(bank)
             for gp in range(4):
-                nc.scalar.copy(out=gwords[:, 512 * gp:512 * (gp + 1)].rearrange("p (w u) -> p w u", u=2),
-                               in_=banks[gp][:].rearrange("p (u w) -> p w u", u=2))
-            cols = slice(1024 * idx, 1024 * (idx + 1))
-            nc.vector.quantize_mx(out=xq[:, cols].bitcast(FP8X4), scales=xs[:, cols], in_=g[:])
+                copy = nc.vector.tensor_copy if gp >= 4 - X_V_BANKS else nc.scalar.copy
+                copy(out=gwords[:, 512 * gp:512 * (gp + 1)].rearrange("p (w u) -> p w u", u=2),
+                     in_=banks[gp][:].rearrange("p (u w) -> p w u", u=2))
 
-        def hidden(tt):
+        hbank = {}
+        hgrouped = {}
+
+        def hidden_matmul(tt):
             bank = psum.tile([P, BANK], F32, name="bank", tag="ps")
             for j in range(4):
                 for gp in range(4):
@@ -128,19 +144,23 @@ def tile_adaptiveinputsoftmax_pa_kernel(tc, x, tail_proj_0, tail_w_0, cluster_pr
                                         lhsT=pq[:, a].bitcast(FP8X4), lhsT_scale=ps[:, a],
                                         rhs=xq[:, b].bitcast(FP8X4), rhs_scale=xs[:, b],
                                         start=(gp == 0), stop=(gp == 3))
+            hbank[tt] = bank
+
+        def hidden_copy(tt):
             g = hgrp.tile([P, 512], BF16, name="hg", tag="hg", align_bytes=64)
             nc.scalar.copy(out=g[:].rearrange("p (w j) -> p w j", j=4),
-                           in_=bank[:].rearrange("p (j w) -> p w j", j=4))
-            cols = slice(128 * tt, 128 * (tt + 1))
-            nc.vector.quantize_mx(out=hq[:, cols].bitcast(FP8X4), scales=hs[:, cols], in_=g[:])
+                           in_=hbank[tt][:].rearrange("p (j w) -> p w j", j=4))
+            hgrouped[tt] = g
 
-        def prep_w(idx):
-            t = loaded[("w", idx)]
-            g = grp.tile([P, 4096], BF16, name="grpt", tag="grp", align_bytes=64)
-            regroup(nc.vector.tensor_copy, g[:], t[:], 0, W_V_COLS)
-            regroup(nc.scalar.copy, g[:], t[:], W_V_COLS, W_CHUNK)
-            cols = slice(W_CHUNK * idx, W_CHUNK * (idx + 1))
-            nc.vector.quantize_mx(out=wq[:, cols].bitcast(FP8X4), scales=ws[:, cols], in_=g[:])
+        def hidden_quantise(tt):
+            cols = slice(128 * tt, 128 * (tt + 1))
+            nc.vector.quantize_mx(out=hq[:, cols].bitcast(FP8X4), scales=hs[:, cols], in_=hgrouped[tt][:])
+
+        def w_regroup(idx):
+            unit = ("w", idx)
+            new_grouped(unit)
+            regroup(nc.vector.tensor_copy, grouped[unit][:], loaded[unit][:], 0, W_V_COLS[idx])
+            regroup(nc.scalar.copy, grouped[unit][:], loaded[unit][:], W_V_COLS[idx], W_CHUNK)
 
         state = {}
 
@@ -148,79 +168,146 @@ def tile_adaptiveinputsoftmax_pa_kernel(tc, x, tail_proj_0, tail_w_0, cluster_pr
             state[tt] = {
                 "nm4": stat.tile([P, 4], F32, name="nm4", tag="nm4"),
                 "s16": stat.tile([P, 16], F32, name="s16", tag="s16"),
-                "e": [],
+                "e": {}, "gm": {}, "bank": {},
             }
 
-        def logits_group(tt, g):
+        def logits(tt, b):
             st = state[tt]
             tcols = slice(128 * tt, 128 * (tt + 1))
-            gm = gstat.tile([P, 4], F32, name="gm", tag="gm")
-            e = epool.tile([P, GROUP], F32, name="e", tag="e")
-            banks = []
-            for i in range(4):
-                bank = psum.tile([P, BANK], F32, name="bank", tag="ps")
-                n = slice(GROUP * g + BANK * i, GROUP * g + BANK * (i + 1))
-                nc.tensor.matmul_mx(out=bank[:], lhsT=hq[:, tcols].bitcast(FP8X4), lhsT_scale=hs[:, tcols],
-                                    rhs=wq[:, n].bitcast(FP8X4), rhs_scale=ws[:, n], start=True, stop=True)
-                banks.append(bank)
-            for i in range(4):
-                nc.vector.tensor_reduce(out=gm[:, i:i + 1], in_=banks[i][:], axis=AX.X, op=ALU.max)
-            nc.vector.tensor_reduce(out=st["nm4"][:, g:g + 1], in_=gm[:], axis=AX.X, op=ALU.max, negate=True)
-            for i in range(4):
-                nc.scalar.activation(out=e[:, BANK * i:BANK * (i + 1)], in_=banks[i][:], func=AF.Exp,
-                                     bias=st["nm4"][:, g:g + 1], scale=1.0,
-                                     accum_out=st["s16"][:, 4 * g + i:4 * g + i + 1])
-            st["e"].append(e)
+            bank = psum.tile([P, BANK], F32, name="bank", tag="ps")
+            n = slice(BANK * b, BANK * (b + 1))
+            nc.tensor.matmul_mx(out=bank[:], lhsT=hq[:, tcols].bitcast(FP8X4), lhsT_scale=hs[:, tcols],
+                                rhs=wq[:, n].bitcast(FP8X4), rhs_scale=ws[:, n], start=True, stop=True)
+            st["bank"][b] = bank
 
-        def finish(tt, engines):
+        def bank_max(tt, b):
             st = state[tt]
-            nmax = stat.tile([P, 1], F32, name="nmax", tag="nmax")
-            nc.vector.tensor_reduce(out=nmax[:], in_=st["nm4"][:], axis=AX.X, op=ALU.min)
-            f4 = stat.tile([P, 4], F32, name="f4", tag="f4")
-            nc.scalar.activation(out=f4[:], in_=st["nm4"][:], func=AF.Exp, bias=nmax[:], scale=-1.0)
+            g, i = b // 4, b % 4
+            if i == 0:
+                st["gm"][g] = gstat.tile([P, 4], F32, name="gm", tag="gm")
+            nc.vector.tensor_reduce(out=st["gm"][g][:, i:i + 1], in_=st["bank"][b][:], axis=AX.X, op=ALU.max)
+            if i == 3:
+                nc.vector.tensor_reduce(out=st["nm4"][:, g:g + 1], in_=st["gm"][g][:], axis=AX.X, op=ALU.max, negate=True)
+
+        def bank_exp(tt, b):
+            st = state[tt]
+            g, i = b // 4, b % 4
+            if i == 0:
+                st["e"][g] = epool.tile([P, GROUP], F32, name="e", tag="e")
+            nc.scalar.activation(out=st["e"][g][:, BANK * i:BANK * (i + 1)], in_=st["bank"][b][:], func=AF.Exp,
+                                 bias=st["nm4"][:, g:g + 1], scale=1.0, accum_out=st["s16"][:, b:b + 1])
+
+        def fin_max(tt):
+            st = state[tt]
+            st["nmax"] = stat.tile([P, 1], F32, name="nmax", tag="nmax")
+            nc.vector.tensor_reduce(out=st["nmax"][:], in_=st["nm4"][:], axis=AX.X, op=ALU.min)
+
+        def fin_factors(tt):
+            st = state[tt]
+            st["f4"] = stat.tile([P, 4], F32, name="f4", tag="f4")
+            nc.scalar.activation(out=st["f4"][:], in_=st["nm4"][:], func=AF.Exp, bias=st["nmax"][:], scale=-1.0)
+
+        def fin_scale(tt):
+            st = state[tt]
             s4 = stat.tile([P, 4], F32, name="s4", tag="s4")
             nc.vector.tensor_reduce(out=s4[:], in_=st["s16"][:].rearrange("p (g i) -> p g i", i=4), axis=AX.X, op=ALU.add)
             fs = stat.tile([P, 4], F32, name="fs", tag="fs")
-            nc.vector.tensor_tensor(out=fs[:], in0=f4[:], in1=s4[:], op=ALU.mult)
+            nc.vector.tensor_tensor(out=fs[:], in0=st["f4"][:], in1=s4[:], op=ALU.mult)
             tot = stat.tile([P, 1], F32, name="tot", tag="tot")
             nc.vector.tensor_reduce(out=tot[:], in_=fs[:], axis=AX.X, op=ALU.add)
             rtot = stat.tile([P, 1], F32, name="rtot", tag="rtot")
             nc.vector.reciprocal(out=rtot[:], in_=tot[:])
-            sc4 = stat.tile([P, 4], F32, name="sc4", tag="sc4")
-            nc.vector.tensor_scalar(out=sc4[:], in0=f4[:], scalar1=rtot[:], scalar2=prob[:, tt:tt + 1],
+            st["sc4"] = stat.tile([P, 4], F32, name="sc4", tag="sc4")
+            nc.vector.tensor_scalar(out=st["sc4"][:], in0=st["f4"][:], scalar1=rtot[:], scalar2=prob[:, tt:tt + 1],
                                     op0=ALU.mult, op1=ALU.mult)
-            for g in range(4):
-                e = st["e"][g]
-                s = sc4[:, g:g + 1]
-                if engines[g] == "g":
-                    nc.gpsimd.tensor_scalar(out=e[:], in0=e[:], scalar1=s, scalar2=0.0, op0=ALU.mult, op1=ALU.add)
-                elif engines[g] == "v":
-                    nc.vector.tensor_scalar(out=e[:], in0=e[:], scalar1=s, scalar2=None, op0=ALU.mult)
-                else:
-                    nc.scalar.activation(out=e[:], in_=e[:], func=AF.Copy, scale=s)
-                nc.sync.dma_start(out=out_rows[128 * tt:128 * (tt + 1), GROUP * g:GROUP * (g + 1)], in_=e[:])
 
-        units = [("proj", 0), ("proj", 1), ("x", 0), ("x", 1)] + [("w", c) for c in range(N_CHUNKS)]
-        for u in units[:RAW_BUFS]:
-            load(u)
-        start_tile(0)
-        for n, unit in enumerate(units):
-            kind, idx = unit
-            if kind == "proj":
-                prep_proj(idx)
-            elif kind == "x":
-                prep_x(idx)
-                hidden(2 * idx)
-                hidden(2 * idx + 1)
+        def scale_store(tt, g, engine, c0=0, c1=GROUP):
+            st = state[tt]
+            e = st["e"][g][:, c0:c1]
+            s = st["sc4"][:, g:g + 1]
+            if engine == "g":
+                nc.gpsimd.tensor_scalar(out=e, in0=e, scalar1=s, scalar2=0.0, op0=ALU.mult, op1=ALU.add)
+            elif engine == "v":
+                nc.vector.tensor_scalar(out=e, in0=e, scalar1=s, scalar2=None, op0=ALU.mult)
             else:
-                prep_w(idx)
-                if idx % 2 == 1:
-                    logits_group(0, idx // 2)
-            if n + RAW_BUFS < len(units):
-                load(units[n + RAW_BUFS])
-        finish(0, "gggg")
+                nc.scalar.activation(out=e, in_=e, func=AF.Copy, scale=s)
+            nc.sync.dma_start(out=out_rows[128 * tt:128 * (tt + 1), GROUP * g + c0:GROUP * g + c1], in_=e)
+
+        for n in range(RAW_BUFS):
+            load_next()
+        prob_bf = keep.tile([P, 4], BF16, name="prob_bf")
+        with nc.allow_non_contiguous_dma(reason="512 two-byte values, one column per token tile"):
+            nc.scalar.dma_start(out=prob_bf[:], in_=prob_cols)
+        prob = keep.tile([P, 4], F32, name="prob")
+
+        proj_regroup(0)
+        load_next()
+        proj_regroup(1)
+        load_next()
+        quantise(("proj", 0))
+        x_transpose(0)
+        load_next()
+        quantise(("proj", 1))
+        x_transpose(1)
+        load_next()
+        quantise(("x", 0))
+        hidden_matmul(0)
+        hidden_matmul(1)
+
+        start_tile(0)
+        exps = []
+        for c in range(N_CHUNKS + 1):
+            if c >= 1:
+                quantise(("w", c - 1))
+                logits(0, 2 * (c - 1))
+                logits(0, 2 * (c - 1) + 1)
+            if c < N_CHUNKS:
+                w_regroup(c)
+                load_next()
+            if c == 0:
+                quantise(("x", 1))
+                hidden_copy(0)
+                hidden_copy(1)
+                hidden_matmul(2)
+                hidden_matmul(3)
+                hidden_quantise(0)
+                nc.vector.tensor_copy(out=prob[:], in_=prob_bf[:])
+            if c == 1:
+                hidden_copy(2)
+                hidden_copy(3)
+                hidden_quantise(1)
+            if c == 2:
+                hidden_quantise(2)
+                hidden_quantise(3)
+            for b in exps[:2]:
+                bank_exp(0, b)
+            exps = exps[2:]
+            if c >= 1:
+                bank_max(0, 2 * (c - 1))
+                bank_max(0, 2 * (c - 1) + 1)
+                if c % 2 == 0:
+                    exps = exps + [2 * c - 4, 2 * c - 3, 2 * c - 2, 2 * c - 1]
+        fin_max(0)
+        fin_factors(0)
+        for b in exps:
+            bank_exp(0, b)
+
         for tt in range(1, 4):
             start_tile(tt)
             for g in range(4):
-                logits_group(tt, g)
-            finish(tt, "gggg" if tt < 3 else "vvsg")
+                for i in range(4):
+                    logits(tt, 4 * g + i)
+                for i in range(4):
+                    bank_max(tt, 4 * g + i)
+                    if 4 * g + i == FIN_LAG:
+                        fin_scale(tt - 1)
+                        for gg in range(4):
+                            scale_store(tt - 1, gg, MID[tt - 1][gg])
+                if g == 3:
+                    fin_max(tt)
+                    fin_factors(tt)
+                for i in range(4):
+                    bank_exp(tt, 4 * g + i)
+        fin_scale(3)
+        for g, engine, c0, c1 in TAIL:
+            scale_store(3, g, engine, c0, c1)

@@ -25,6 +25,11 @@ GROUP = 2048
 BANK = 512
 
 RAW_BUFS = 5
+GB = 4
+NG = 16 // GB
+GCOLS = BANK * GB
+M_LAG = 2
+E_LAG = 2
 W_V_COLS = [448] * 8
 PROJ_V_COLS = 256
 X_V_BANKS = 1
@@ -52,7 +57,7 @@ def tile_adaptiveinputsoftmax_pa_kernel(tc, x, tail_proj_0, tail_w_0, cluster_pr
         raw = ctx.enter_context(tc.tile_pool(name="raw", bufs=RAW_BUFS))
         grp = ctx.enter_context(tc.tile_pool(name="grp", bufs=3))
         hgrp = ctx.enter_context(tc.tile_pool(name="hgrp", bufs=2))
-        epool = ctx.enter_context(tc.tile_pool(name="epool", bufs=12))
+        epool = ctx.enter_context(tc.tile_pool(name="epool", bufs=12 * 4 // GB))
         stat = ctx.enter_context(tc.tile_pool(name="stat", bufs=4))
         gstat = ctx.enter_context(tc.tile_pool(name="gstat", bufs=4))
         psum = ctx.enter_context(tc.psum_pool(name="psum", bufs=8))
@@ -76,7 +81,7 @@ def tile_adaptiveinputsoftmax_pa_kernel(tc, x, tail_proj_0, tail_w_0, cluster_pr
 
         loaded = {}
         grouped = {}
-        units = [("proj", 0), ("proj", 1), ("x", 0), ("x", 1)] + [("w", c) for c in range(N_CHUNKS)]
+        units = [("x", 0), ("proj", 0), ("proj", 1), ("x", 1)] + [("w", c) for c in range(N_CHUNKS)]
         queue = list(units)
 
         def load_next():
@@ -111,6 +116,8 @@ def tile_adaptiveinputsoftmax_pa_kernel(tc, x, tail_proj_0, tail_w_0, cluster_pr
             cols = slice(1024 * idx, 1024 * (idx + 1))
             nc.vector.quantize_mx(out=codes[:, cols].bitcast(FP8X4), scales=scales[:, cols], in_=grouped[unit][:])
 
+        xbanks = {}
+
         def x_transpose(idx):
             unit = ("x", idx)
             new_grouped(unit)
@@ -125,6 +132,12 @@ def tile_adaptiveinputsoftmax_pa_kernel(tc, x, tail_proj_0, tail_w_0, cluster_pr
                         nc.tensor.transpose(out=bank[:, 256 * u + 128 * i:256 * u + 128 * (i + 1)],
                                             in_=words[:, src0:src0 + 128], identity=ident[:])
                 banks.append(bank)
+            xbanks[idx] = banks
+
+        def x_copy(idx):
+            unit = ("x", idx)
+            gwords = grouped[unit][:].bitcast(F32)
+            banks = xbanks[idx]
             for gp in range(4):
                 copy = nc.vector.tensor_copy if gp >= 4 - X_V_BANKS else nc.scalar.copy
                 copy(out=gwords[:, 512 * gp:512 * (gp + 1)].rearrange("p (w u) -> p w u", u=2),
@@ -166,7 +179,7 @@ def tile_adaptiveinputsoftmax_pa_kernel(tc, x, tail_proj_0, tail_w_0, cluster_pr
 
         def start_tile(tt):
             state[tt] = {
-                "nm4": stat.tile([P, 4], F32, name="nm4", tag="nm4"),
+                "nm4": stat.tile([P, NG], F32, name="nm4", tag="nm4"),
                 "s16": stat.tile([P, 16], F32, name="s16", tag="s16"),
                 "e": {}, "gm": {}, "bank": {},
             }
@@ -182,18 +195,18 @@ def tile_adaptiveinputsoftmax_pa_kernel(tc, x, tail_proj_0, tail_w_0, cluster_pr
 
         def bank_max(tt, b):
             st = state[tt]
-            g, i = b // 4, b % 4
+            g, i = b // GB, b % GB
             if i == 0:
-                st["gm"][g] = gstat.tile([P, 4], F32, name="gm", tag="gm")
+                st["gm"][g] = gstat.tile([P, GB], F32, name="gm", tag="gm")
             nc.vector.tensor_reduce(out=st["gm"][g][:, i:i + 1], in_=st["bank"][b][:], axis=AX.X, op=ALU.max)
-            if i == 3:
+            if i == GB - 1:
                 nc.vector.tensor_reduce(out=st["nm4"][:, g:g + 1], in_=st["gm"][g][:], axis=AX.X, op=ALU.max, negate=True)
 
         def bank_exp(tt, b):
             st = state[tt]
-            g, i = b // 4, b % 4
+            g, i = b // GB, b % GB
             if i == 0:
-                st["e"][g] = epool.tile([P, GROUP], F32, name="e", tag="e")
+                st["e"][g] = epool.tile([P, GCOLS], F32, name="e", tag="e")
             nc.scalar.activation(out=st["e"][g][:, BANK * i:BANK * (i + 1)], in_=st["bank"][b][:], func=AF.Exp,
                                  bias=st["nm4"][:, g:g + 1], scale=1.0, accum_out=st["s16"][:, b:b + 1])
 
@@ -204,24 +217,24 @@ def tile_adaptiveinputsoftmax_pa_kernel(tc, x, tail_proj_0, tail_w_0, cluster_pr
 
         def fin_factors(tt):
             st = state[tt]
-            st["f4"] = stat.tile([P, 4], F32, name="f4", tag="f4")
+            st["f4"] = stat.tile([P, NG], F32, name="f4", tag="f4")
             nc.scalar.activation(out=st["f4"][:], in_=st["nm4"][:], func=AF.Exp, bias=st["nmax"][:], scale=-1.0)
 
         def fin_scale(tt):
             st = state[tt]
-            s4 = stat.tile([P, 4], F32, name="s4", tag="s4")
-            nc.vector.tensor_reduce(out=s4[:], in_=st["s16"][:].rearrange("p (g i) -> p g i", i=4), axis=AX.X, op=ALU.add)
-            fs = stat.tile([P, 4], F32, name="fs", tag="fs")
+            s4 = stat.tile([P, NG], F32, name="s4", tag="s4")
+            nc.vector.tensor_reduce(out=s4[:], in_=st["s16"][:].rearrange("p (g i) -> p g i", i=GB), axis=AX.X, op=ALU.add)
+            fs = stat.tile([P, NG], F32, name="fs", tag="fs")
             nc.vector.tensor_tensor(out=fs[:], in0=st["f4"][:], in1=s4[:], op=ALU.mult)
             tot = stat.tile([P, 1], F32, name="tot", tag="tot")
             nc.vector.tensor_reduce(out=tot[:], in_=fs[:], axis=AX.X, op=ALU.add)
             rtot = stat.tile([P, 1], F32, name="rtot", tag="rtot")
             nc.vector.reciprocal(out=rtot[:], in_=tot[:])
-            st["sc4"] = stat.tile([P, 4], F32, name="sc4", tag="sc4")
+            st["sc4"] = stat.tile([P, NG], F32, name="sc4", tag="sc4")
             nc.vector.tensor_scalar(out=st["sc4"][:], in0=st["f4"][:], scalar1=rtot[:], scalar2=prob[:, tt:tt + 1],
                                     op0=ALU.mult, op1=ALU.mult)
 
-        def scale_store(tt, g, engine, c0=0, c1=GROUP):
+        def scale_store(tt, g, engine, c0=0, c1=GCOLS):
             st = state[tt]
             e = st["e"][g][:, c0:c1]
             s = st["sc4"][:, g:g + 1]
@@ -231,33 +244,32 @@ def tile_adaptiveinputsoftmax_pa_kernel(tc, x, tail_proj_0, tail_w_0, cluster_pr
                 nc.vector.tensor_scalar(out=e, in0=e, scalar1=s, scalar2=None, op0=ALU.mult)
             else:
                 nc.scalar.activation(out=e, in_=e, func=AF.Copy, scale=s)
-            nc.sync.dma_start(out=out_rows[128 * tt:128 * (tt + 1), GROUP * g + c0:GROUP * g + c1], in_=e)
+            nc.sync.dma_start(out=out_rows[128 * tt:128 * (tt + 1), GCOLS * g + c0:GCOLS * g + c1], in_=e)
 
         for n in range(RAW_BUFS):
             load_next()
         prob_bf = keep.tile([P, 4], BF16, name="prob_bf")
-        with nc.allow_non_contiguous_dma(reason="512 two-byte values, one column per token tile"):
-            nc.scalar.dma_start(out=prob_bf[:], in_=prob_cols)
         prob = keep.tile([P, 4], F32, name="prob")
 
+        x_transpose(0)
+        x_copy(0)
+        load_next()
         proj_regroup(0)
         load_next()
+        quantise(("x", 0))
         proj_regroup(1)
         load_next()
         quantise(("proj", 0))
-        x_transpose(0)
-        load_next()
-        quantise(("proj", 1))
         x_transpose(1)
-        load_next()
-        quantise(("x", 0))
+        quantise(("proj", 1))
         hidden_matmul(0)
         hidden_matmul(1)
+        x_copy(1)
+        load_next()
 
         start_tile(0)
-        exps = []
-        for c in range(N_CHUNKS + 1):
-            if c >= 1:
+        for c in range(N_CHUNKS + M_LAG + E_LAG + 1):
+            if 1 <= c <= N_CHUNKS:
                 quantise(("w", c - 1))
                 logits(0, 2 * (c - 1))
                 logits(0, 2 * (c - 1) + 1)
@@ -271,7 +283,6 @@ def tile_adaptiveinputsoftmax_pa_kernel(tc, x, tail_proj_0, tail_w_0, cluster_pr
                 hidden_matmul(2)
                 hidden_matmul(3)
                 hidden_quantise(0)
-                nc.vector.tensor_copy(out=prob[:], in_=prob_bf[:])
             if c == 1:
                 hidden_copy(2)
                 hidden_copy(3)
@@ -279,35 +290,40 @@ def tile_adaptiveinputsoftmax_pa_kernel(tc, x, tail_proj_0, tail_w_0, cluster_pr
             if c == 2:
                 hidden_quantise(2)
                 hidden_quantise(3)
-            for b in exps[:2]:
-                bank_exp(0, b)
-            exps = exps[2:]
-            if c >= 1:
-                bank_max(0, 2 * (c - 1))
-                bank_max(0, 2 * (c - 1) + 1)
-                if c % 2 == 0:
-                    exps = exps + [2 * c - 4, 2 * c - 3, 2 * c - 2, 2 * c - 1]
-        fin_max(0)
-        fin_factors(0)
-        for b in exps:
-            bank_exp(0, b)
+            if c == N_CHUNKS - 1:
+                with nc.allow_non_contiguous_dma(reason="512 two-byte values, one column per token tile"):
+                    nc.sync.dma_start(out=prob_bf[:], in_=prob_cols)
+            if c == N_CHUNKS + 1:
+                nc.vector.tensor_copy(out=prob[:], in_=prob_bf[:])
+            d = c - M_LAG - E_LAG
+            if 0 <= d < N_CHUNKS:
+                if d == N_CHUNKS - 1:
+                    fin_factors(0)
+                bank_exp(0, 2 * d)
+                bank_exp(0, 2 * d + 1)
+            d = c - M_LAG
+            if 0 <= d < N_CHUNKS:
+                bank_max(0, 2 * d)
+                bank_max(0, 2 * d + 1)
+                if d == N_CHUNKS - 1:
+                    fin_max(0)
 
         for tt in range(1, 4):
             start_tile(tt)
-            for g in range(4):
-                for i in range(4):
-                    logits(tt, 4 * g + i)
-                for i in range(4):
-                    bank_max(tt, 4 * g + i)
-                    if 4 * g + i == FIN_LAG:
+            for g in range(NG):
+                for i in range(GB):
+                    logits(tt, GB * g + i)
+                for i in range(GB):
+                    bank_max(tt, GB * g + i)
+                    if GB * g + i == FIN_LAG:
                         fin_scale(tt - 1)
-                        for gg in range(4):
+                        for gg in range(NG):
                             scale_store(tt - 1, gg, MID[tt - 1][gg])
-                if g == 3:
+                if g == NG - 1:
                     fin_max(tt)
                     fin_factors(tt)
-                for i in range(4):
-                    bank_exp(tt, 4 * g + i)
+                for i in range(GB):
+                    bank_exp(tt, GB * g + i)
         fin_scale(3)
         for g, engine, c0, c1 in TAIL:
             scale_store(3, g, engine, c0, c1)

@@ -25,17 +25,16 @@ GROUP = 2048
 BANK = 512
 
 RAW_BUFS = 5
-GB = 4
-NG = 16 // GB
-GCOLS = BANK * GB
-M_LAG = 2
-E_LAG = 2
+E_BUFS = 12
+NG = 4
 W_V_COLS = [448] * 8
 PROJ_V_COLS = 256
 X_V_BANKS = 1
 TAIL = [(0, "v", 0, 512), (0, "v", 512, 2048), (3, "s", 0, 2048), (1, "v", 0, 2048), (2, "v", 0, 2048)]
-FIN_LAG = 4
-MID = ["gggg", "gggg", "gggg"]
+FIN_LAG = 1
+M_LAG = 2
+MID = ["gggg", "gggg", "ggvv"]
+X_SPLIT = 1
 
 
 def regroup(copy, dst, src, col0, col1):
@@ -57,7 +56,7 @@ def tile_adaptiveinputsoftmax_pa_kernel(tc, x, tail_proj_0, tail_w_0, cluster_pr
         raw = ctx.enter_context(tc.tile_pool(name="raw", bufs=RAW_BUFS))
         grp = ctx.enter_context(tc.tile_pool(name="grp", bufs=3))
         hgrp = ctx.enter_context(tc.tile_pool(name="hgrp", bufs=2))
-        epool = ctx.enter_context(tc.tile_pool(name="epool", bufs=12 * 4 // GB))
+        epool = ctx.enter_context(tc.tile_pool(name="epool", bufs=E_BUFS))
         stat = ctx.enter_context(tc.tile_pool(name="stat", bufs=4))
         gstat = ctx.enter_context(tc.tile_pool(name="gstat", bufs=4))
         psum = ctx.enter_context(tc.psum_pool(name="psum", bufs=8))
@@ -78,11 +77,12 @@ def tile_adaptiveinputsoftmax_pa_kernel(tc, x, tail_proj_0, tail_w_0, cluster_pr
         hs = keep.tile([P, TOK], U8, name="hs", align_bytes=64)
         wq = keep.tile([P, V0], U32, name="wq", align_bytes=64)
         ws = keep.tile([P, V0], U8, name="ws", align_bytes=64)
+        prob_bf = keep.tile([P, 4], BF16, name="prob_bf")
+        prob = keep.tile([P, 4], F32, name="prob")
 
         loaded = {}
         grouped = {}
-        units = [("x", 0), ("proj", 0), ("proj", 1), ("x", 1)] + [("w", c) for c in range(N_CHUNKS)]
-        queue = list(units)
+        queue = [("x", 0), ("proj", 0), ("proj", 1), ("x", 1)] + [("w", c) for c in range(N_CHUNKS)]
 
         def load_next():
             if not queue:
@@ -93,10 +93,23 @@ def tile_adaptiveinputsoftmax_pa_kernel(tc, x, tail_proj_0, tail_w_0, cluster_pr
             if kind == "proj":
                 nc.sync.dma_start(out=t[:].rearrange("p (a f) -> p a f", a=4), in_=proj_rows[:, 4 * idx:4 * idx + 4, :])
             elif kind == "x":
-                nc.sync.dma_start(out=t[:].rearrange("p (i k) -> p i k", i=2), in_=x_rows[:, 2 * idx:2 * idx + 2, :])
+                pieces = X_SPLIT if idx == 0 else 1
+                w = H // pieces
+                for q in range(pieces):
+                    nc.sync.dma_start(out=t[:].rearrange("p (i k) -> p i k", i=2)[:, :, w * q:w * (q + 1)],
+                                      in_=x_rows[:, 2 * idx:2 * idx + 2, w * q:w * (q + 1)])
             else:
                 nc.sync.dma_start(out=t[:].rearrange("p (j n) -> p j n", j=4), in_=w_rows[:, :, W_CHUNK * idx:W_CHUNK * (idx + 1)])
             loaded[unit] = t
+
+        urgent = []
+        pending = []
+
+        def tick():
+            if urgent:
+                urgent.pop(0)()
+            elif pending:
+                pending.pop(0)()
 
         def new_grouped(unit):
             grouped[unit] = grp.tile([P, 4096], BF16, name="grpt", tag="grp", align_bytes=64)
@@ -107,14 +120,14 @@ def tile_adaptiveinputsoftmax_pa_kernel(tc, x, tail_proj_0, tail_w_0, cluster_pr
             for gl in range(2):
                 sl = slice(2048 * gl, 2048 * (gl + 1))
                 regroup(nc.vector.tensor_copy, grouped[unit][:, sl], loaded[unit][:, sl], 0, PROJ_V_COLS)
-                if PROJ_V_COLS < P0:
-                    regroup(nc.scalar.copy, grouped[unit][:, sl], loaded[unit][:, sl], PROJ_V_COLS, P0)
+                regroup(nc.scalar.copy, grouped[unit][:, sl], loaded[unit][:, sl], PROJ_V_COLS, P0)
 
         def quantise(unit):
             kind, idx = unit
             codes, scales = {"proj": (pq, ps), "x": (xq, xs), "w": (wq, ws)}[kind]
             cols = slice(1024 * idx, 1024 * (idx + 1))
             nc.vector.quantize_mx(out=codes[:, cols].bitcast(FP8X4), scales=scales[:, cols], in_=grouped[unit][:])
+            tick()
 
         xbanks = {}
 
@@ -122,7 +135,6 @@ def tile_adaptiveinputsoftmax_pa_kernel(tc, x, tail_proj_0, tail_w_0, cluster_pr
             unit = ("x", idx)
             new_grouped(unit)
             words = loaded[unit][:].bitcast(F32)
-            gwords = grouped[unit][:].bitcast(F32)
             banks = []
             for gp in range(4):
                 bank = psum.tile([P, BANK], F32, name="bank", tag="ps")
@@ -135,13 +147,11 @@ def tile_adaptiveinputsoftmax_pa_kernel(tc, x, tail_proj_0, tail_w_0, cluster_pr
             xbanks[idx] = banks
 
         def x_copy(idx):
-            unit = ("x", idx)
-            gwords = grouped[unit][:].bitcast(F32)
-            banks = xbanks[idx]
+            gwords = grouped[("x", idx)][:].bitcast(F32)
             for gp in range(4):
                 copy = nc.vector.tensor_copy if gp >= 4 - X_V_BANKS else nc.scalar.copy
                 copy(out=gwords[:, 512 * gp:512 * (gp + 1)].rearrange("p (w u) -> p w u", u=2),
-                     in_=banks[gp][:].rearrange("p (u w) -> p w u", u=2))
+                     in_=xbanks[idx][gp][:].rearrange("p (u w) -> p w u", u=2))
 
         hbank = {}
         hgrouped = {}
@@ -173,9 +183,11 @@ def tile_adaptiveinputsoftmax_pa_kernel(tc, x, tail_proj_0, tail_w_0, cluster_pr
             unit = ("w", idx)
             new_grouped(unit)
             regroup(nc.vector.tensor_copy, grouped[unit][:], loaded[unit][:], 0, W_V_COLS[idx])
+            tick()
             regroup(nc.scalar.copy, grouped[unit][:], loaded[unit][:], W_V_COLS[idx], W_CHUNK)
 
         state = {}
+        exp_ready = []
 
         def start_tile(tt):
             state[tt] = {
@@ -193,48 +205,66 @@ def tile_adaptiveinputsoftmax_pa_kernel(tc, x, tail_proj_0, tail_w_0, cluster_pr
                                 rhs=wq[:, n].bitcast(FP8X4), rhs_scale=ws[:, n], start=True, stop=True)
             st["bank"][b] = bank
 
-        def bank_max(tt, b):
+        def group_max(tt, g, now):
             st = state[tt]
-            g, i = b // GB, b % GB
-            if i == 0:
-                st["gm"][g] = gstat.tile([P, GB], F32, name="gm", tag="gm")
-            nc.vector.tensor_reduce(out=st["gm"][g][:, i:i + 1], in_=st["bank"][b][:], axis=AX.X, op=ALU.max)
-            if i == GB - 1:
-                nc.vector.tensor_reduce(out=st["nm4"][:, g:g + 1], in_=st["gm"][g][:], axis=AX.X, op=ALU.max, negate=True)
+            nc.vector.tensor_reduce(out=st["nm4"][:, g:g + 1], in_=st["gm"][g][:], axis=AX.X, op=ALU.max, negate=True)
+            for b in range(4 * g, 4 * g + 4):
+                exp_ready.append((tt, b))
+            if now and g < NG - 1:
+                run_exps(4)
 
-        def bank_exp(tt, b):
+        def bank_max(tt, b, now):
             st = state[tt]
-            g, i = b // GB, b % GB
+            g, i = b // 4, b % 4
             if i == 0:
-                st["e"][g] = epool.tile([P, GCOLS], F32, name="e", tag="e")
-            nc.scalar.activation(out=st["e"][g][:, BANK * i:BANK * (i + 1)], in_=st["bank"][b][:], func=AF.Exp,
-                                 bias=st["nm4"][:, g:g + 1], scale=1.0, accum_out=st["s16"][:, b:b + 1])
+                st["gm"][g] = gstat.tile([P, 4], F32, name="gm", tag="gm")
+            nc.vector.tensor_reduce(out=st["gm"][g][:, i:i + 1], in_=st["bank"][b][:], axis=AX.X, op=ALU.max)
+            tick()
+            if i == 3:
+                urgent.append(lambda: group_max(tt, g, now))
+                if g == NG - 1:
+                    urgent.append(lambda: fin_max(tt))
+
+        def run_exps(count):
+            for n in range(min(count, len(exp_ready))):
+                tt, b = exp_ready.pop(0)
+                st = state[tt]
+                g, i = b // 4, b % 4
+                if i == 0:
+                    st["e"][g] = epool.tile([P, GROUP], F32, name="e", tag="e")
+                nc.scalar.activation(out=st["e"][g][:, BANK * i:BANK * (i + 1)], in_=st["bank"][b][:], func=AF.Exp,
+                                     bias=st["nm4"][:, g:g + 1], scale=1.0, accum_out=st["s16"][:, b:b + 1])
 
         def fin_max(tt):
             st = state[tt]
             st["nmax"] = stat.tile([P, 1], F32, name="nmax", tag="nmax")
             nc.vector.tensor_reduce(out=st["nmax"][:], in_=st["nm4"][:], axis=AX.X, op=ALU.min)
-
-        def fin_factors(tt):
-            st = state[tt]
             st["f4"] = stat.tile([P, NG], F32, name="f4", tag="f4")
             nc.scalar.activation(out=st["f4"][:], in_=st["nm4"][:], func=AF.Exp, bias=st["nmax"][:], scale=-1.0)
+            if tt > 0:
+                run_exps(4)
 
-        def fin_scale(tt):
+        def fin_steps(tt, after):
             st = state[tt]
-            s4 = stat.tile([P, NG], F32, name="s4", tag="s4")
-            nc.vector.tensor_reduce(out=s4[:], in_=st["s16"][:].rearrange("p (g i) -> p g i", i=GB), axis=AX.X, op=ALU.add)
-            fs = stat.tile([P, NG], F32, name="fs", tag="fs")
-            nc.vector.tensor_tensor(out=fs[:], in0=st["f4"][:], in1=s4[:], op=ALU.mult)
-            tot = stat.tile([P, 1], F32, name="tot", tag="tot")
-            nc.vector.tensor_reduce(out=tot[:], in_=fs[:], axis=AX.X, op=ALU.add)
+            junk = stat.tile([P, 4], F32, name="junk", tag="junk")
+            acc = stat.tile([P, NG], F32, name="acc", tag="acc")
             rtot = stat.tile([P, 1], F32, name="rtot", tag="rtot")
-            nc.vector.reciprocal(out=rtot[:], in_=tot[:])
             st["sc4"] = stat.tile([P, NG], F32, name="sc4", tag="sc4")
-            nc.vector.tensor_scalar(out=st["sc4"][:], in0=st["f4"][:], scalar1=rtot[:], scalar2=prob[:, tt:tt + 1],
-                                    op0=ALU.mult, op1=ALU.mult)
 
-        def scale_store(tt, g, engine, c0=0, c1=GCOLS):
+            def add_group(g):
+                nc.vector.tensor_scalar(out=junk[:], in0=st["s16"][:, 4 * g:4 * g + 4], scalar1=st["f4"][:, g:g + 1],
+                                        scalar2=(acc[:, g - 1:g] if g else 0.0), op0=ALU.mult, op1=ALU.add,
+                                        accum_out=acc[:, g:g + 1])
+
+            def last():
+                nc.vector.reciprocal(out=rtot[:], in_=acc[:, NG - 1:NG])
+                FIN_ENGINE[tt].tensor_scalar(out=st["sc4"][:], in0=st["f4"][:], scalar1=rtot[:], scalar2=prob[:, tt:tt + 1],
+                                             op0=ALU.mult, op1=ALU.mult)
+                after()
+
+            return [lambda: add_group(0), lambda: add_group(1), lambda: add_group(2), lambda: add_group(3), last]
+
+        def scale_store(tt, g, engine, c0=0, c1=GROUP):
             st = state[tt]
             e = st["e"][g][:, c0:c1]
             s = st["sc4"][:, g:g + 1]
@@ -244,13 +274,20 @@ def tile_adaptiveinputsoftmax_pa_kernel(tc, x, tail_proj_0, tail_w_0, cluster_pr
                 nc.vector.tensor_scalar(out=e, in0=e, scalar1=s, scalar2=None, op0=ALU.mult)
             else:
                 nc.scalar.activation(out=e, in_=e, func=AF.Copy, scale=s)
-            nc.sync.dma_start(out=out_rows[128 * tt:128 * (tt + 1), GCOLS * g + c0:GCOLS * g + c1], in_=e)
+            nc.sync.dma_start(out=out_rows[128 * tt:128 * (tt + 1), GROUP * g + c0:GROUP * g + c1], in_=e)
+
+        FIN_ENGINE = [nc.gpsimd, nc.gpsimd, nc.gpsimd, nc.vector]
+        late = []
+
+        def gpsimd_scales(tt):
+            for g in range(NG):
+                if MID[tt][g] == "g":
+                    scale_store(tt, g, "g")
+                else:
+                    late.append((tt, g, MID[tt][g]))
 
         for n in range(RAW_BUFS):
             load_next()
-        prob_bf = keep.tile([P, 4], BF16, name="prob_bf")
-        prob = keep.tile([P, 4], F32, name="prob")
-
         x_transpose(0)
         x_copy(0)
         load_next()
@@ -268,7 +305,7 @@ def tile_adaptiveinputsoftmax_pa_kernel(tc, x, tail_proj_0, tail_w_0, cluster_pr
         load_next()
 
         start_tile(0)
-        for c in range(N_CHUNKS + M_LAG + E_LAG + 1):
+        for c in range(N_CHUNKS + M_LAG):
             if 1 <= c <= N_CHUNKS:
                 quantise(("w", c - 1))
                 logits(0, 2 * (c - 1))
@@ -295,35 +332,31 @@ def tile_adaptiveinputsoftmax_pa_kernel(tc, x, tail_proj_0, tail_w_0, cluster_pr
                     nc.sync.dma_start(out=prob_bf[:], in_=prob_cols)
             if c == N_CHUNKS + 1:
                 nc.vector.tensor_copy(out=prob[:], in_=prob_bf[:])
-            d = c - M_LAG - E_LAG
-            if 0 <= d < N_CHUNKS:
-                if d == N_CHUNKS - 1:
-                    fin_factors(0)
-                bank_exp(0, 2 * d)
-                bank_exp(0, 2 * d + 1)
+            run_exps(2)
             d = c - M_LAG
-            if 0 <= d < N_CHUNKS:
-                bank_max(0, 2 * d)
-                bank_max(0, 2 * d + 1)
-                if d == N_CHUNKS - 1:
-                    fin_max(0)
+            if d >= 0:
+                bank_max(0, 2 * d, False)
+                bank_max(0, 2 * d + 1, False)
 
         for tt in range(1, 4):
             start_tile(tt)
-            for g in range(NG):
-                for i in range(GB):
-                    logits(tt, GB * g + i)
-                for i in range(GB):
-                    bank_max(tt, GB * g + i)
-                    if GB * g + i == FIN_LAG:
-                        fin_scale(tt - 1)
-                        for gg in range(NG):
-                            scale_store(tt - 1, gg, MID[tt - 1][gg])
-                if g == NG - 1:
-                    fin_max(tt)
-                    fin_factors(tt)
-                for i in range(GB):
-                    bank_exp(tt, GB * g + i)
-        fin_scale(3)
-        for g, engine, c0, c1 in TAIL:
-            scale_store(3, g, engine, c0, c1)
+            for b in range(16):
+                if b % 4 == 0:
+                    for i in range(4):
+                        logits(tt, b + i)
+                bank_max(tt, b, True)
+                if tt == 1 and b < 2:
+                    run_exps(4)
+                if b == FIN_LAG:
+                    pending.extend(fin_steps(tt - 1, lambda: gpsimd_scales(tt - 1)))
+        while urgent or pending:
+            tick()
+        for tt, g, engine in late:
+            scale_store(tt, g, {"v": "v", "G": "g", "s": "s"}[engine])
+
+        def tail():
+            for g, engine, c0, c1 in TAIL:
+                scale_store(3, g, engine, c0, c1)
+
+        for step in fin_steps(3, tail):
+            step()

@@ -13,33 +13,40 @@ ALU = mybir.AluOpType
 AX = mybir.AxisListType
 
 P = 128
-TOK = 512
+TOKENS = 512
 H = 2048
 P0 = 512
 V0 = 8192
-FLOPS = 2 * TOK * H * P0 + 2 * TOK * P0 * V0
+FLOPS = 2 * TOKENS * H * P0 + 2 * TOKENS * P0 * V0
 
-W_CHUNK = 1024
-N_CHUNKS = V0 // W_CHUNK
-GROUP = 2048
+PACK = 4
+PASSES = H // (P * PACK)
+PASS_PAIRS = P * PACK // 2
+TILES = TOKENS // P
 BANK = 512
+BANKS = V0 // BANK
+GROUP_BANKS = 4
+GROUP = GROUP_BANKS * BANK
+GROUPS = V0 // GROUP
+LOAD = 4096
+WORDS = LOAD // PACK
+LOAD_TOKENS = LOAD // H * P
+CHUNKS = P0 * V0 // (P * LOAD)
+CHUNK_BANKS = WORDS // BANK
+RUN = 4
 
-RAW_BUFS = 5
-E_BUFS = 12
-NG = 4
-W_V_COLS = [448] * 8
-PROJ_V_COLS = 256
-X_V_BANKS = 1
-TAIL = [(0, "v", 0, 512), (0, "v", 512, 2048), (3, "s", 0, 2048), (1, "v", 0, 2048), (2, "v", 0, 2048)]
-FIN_LAG = 1
-M_LAG = 2
-MID = ["gggg", "gggg", "ggvv"]
-X_SPLIT = 1
+LOADS_AHEAD = 5
+PROJ_VECTOR_COLS = 256
+W_VECTOR_COLS = [576, 576] + [416] * (CHUNKS - 2)
+X_VECTOR_BANKS = 1
+MAX_LAG = 2
+TOTAL_BEHIND_BANK = [4, 1, 1]
+GPSIMD_GROUPS = [4, 4, 1]
 
 
-def regroup(copy, dst, src, col0, col1):
-    d = dst.rearrange("p (c i t) -> p c t i", i=4, t=4)[:, col0 // 4:col1 // 4, :, :]
-    s = src.rearrange("p (t c i) -> p c t i", t=4, i=4)[:, col0 // 4:col1 // 4, :, :]
+def regroup(copy, dst, src, first, last):
+    d = dst.rearrange("p (c i t) -> p c t i", i=RUN, t=PACK)[:, first // RUN:last // RUN, :, :]
+    s = src.rearrange("p (t c i) -> p c t i", t=PACK, i=RUN)[:, first // RUN:last // RUN, :, :]
     copy(out=d, in_=s)
 
 
@@ -47,316 +54,304 @@ def tile_adaptiveinputsoftmax_pa_kernel(tc, x, tail_proj_0, tail_w_0, cluster_pr
     nc = tc.nc
     x_rows = x.rearrange("n t h -> (n t) h").rearrange("(i p) k -> p i k", p=P)
     proj_rows = tail_proj_0.rearrange("(a p e) n -> p a (e n)", p=P, e=2)
-    w_rows = tail_w_0.rearrange("(j p) n -> p j n", p=P)
+    w_rows = tail_w_0.rearrange("(t p) n -> p t n", p=P)
     out_rows = out.rearrange("n t v -> (n t) v")
-    prob_cols = cluster_prob.rearrange("n t o -> (n t o)").rearrange("(c p) -> p c", p=P)
+    prob_cols = cluster_prob.rearrange("n t o -> (n t o)").rearrange("(i p) -> p i", p=P)
 
     with ExitStack() as ctx:
         keep = ctx.enter_context(tc.tile_pool(name="keep", bufs=1))
-        raw = ctx.enter_context(tc.tile_pool(name="raw", bufs=RAW_BUFS))
-        grp = ctx.enter_context(tc.tile_pool(name="grp", bufs=3))
-        hgrp = ctx.enter_context(tc.tile_pool(name="hgrp", bufs=2))
-        epool = ctx.enter_context(tc.tile_pool(name="epool", bufs=E_BUFS))
-        stat = ctx.enter_context(tc.tile_pool(name="stat", bufs=4))
-        gstat = ctx.enter_context(tc.tile_pool(name="gstat", bufs=4))
+        raw_pool = ctx.enter_context(tc.tile_pool(name="raw", bufs=LOADS_AHEAD))
+        grouped_pool = ctx.enter_context(tc.tile_pool(name="grouped", bufs=3))
+        h_pool = ctx.enter_context(tc.tile_pool(name="h", bufs=2))
+        numerator_pool = ctx.enter_context(tc.tile_pool(name="numerators", bufs=3 * GROUPS))
+        row_pool = ctx.enter_context(tc.tile_pool(name="row", bufs=TILES))
+        maxima_pool = ctx.enter_context(tc.tile_pool(name="maxima", bufs=GROUPS))
         psum = ctx.enter_context(tc.psum_pool(name="psum", bufs=8))
         ctx.enter_context(tc.manual_schedule())
 
-        ident = keep.tile([P, P], F32, name="ident")
-        make_identity(nc, ident[:])
-        warm = keep.tile([P, 1], F32, name="warm")
-        nc.vector.memset(warm[:], 0.0)
-        warm2 = keep.tile([P, 1], F32, name="warm2")
-        nc.scalar.activation(out=warm2[:], in_=warm[:], func=AF.Exp)
+        identity = keep.tile([P, P], F32, name="identity")
+        make_identity(nc, identity[:])
+        zero = keep.tile([P, 1], F32, name="zero")
+        nc.vector.memset(zero[:], 0.0)
+        one = keep.tile([P, 1], F32, name="one")
+        nc.scalar.activation(out=one[:], in_=zero[:], func=AF.Exp)
 
-        pq = keep.tile([P, 4 * P0], U32, name="pq", align_bytes=64)
-        ps = keep.tile([P, 4 * P0], U8, name="ps", align_bytes=64)
-        xq = keep.tile([P, 4 * TOK], U32, name="xq", align_bytes=64)
-        xs = keep.tile([P, 4 * TOK], U8, name="xs", align_bytes=64)
-        hq = keep.tile([P, TOK], U32, name="hq", align_bytes=64)
-        hs = keep.tile([P, TOK], U8, name="hs", align_bytes=64)
-        wq = keep.tile([P, V0], U32, name="wq", align_bytes=64)
-        ws = keep.tile([P, V0], U8, name="ws", align_bytes=64)
-        prob_bf = keep.tile([P, 4], BF16, name="prob_bf")
-        prob = keep.tile([P, 4], F32, name="prob")
+        proj_words = keep.tile([P, PASSES * P0], U32, name="proj_words", align_bytes=64)
+        proj_scales = keep.tile([P, PASSES * P0], U8, name="proj_scales", align_bytes=64)
+        x_words = keep.tile([P, PASSES * TOKENS], U32, name="x_words", align_bytes=64)
+        x_scales = keep.tile([P, PASSES * TOKENS], U8, name="x_scales", align_bytes=64)
+        h_words = keep.tile([P, TOKENS], U32, name="h_words", align_bytes=64)
+        h_scales = keep.tile([P, TOKENS], U8, name="h_scales", align_bytes=64)
+        w_words = keep.tile([P, V0], U32, name="w_words", align_bytes=64)
+        w_scales = keep.tile([P, V0], U8, name="w_scales", align_bytes=64)
+        operands = {"proj": (proj_words, proj_scales), "x": (x_words, x_scales), "w": (w_words, w_scales)}
+        prob_bf16 = keep.tile([P, TILES], BF16, name="prob_bf16")
+        prob = keep.tile([P, TILES], F32, name="prob")
 
-        loaded = {}
+        to_load = [("x", 0), ("proj", 0), ("proj", 1), ("x", 1)] + [("w", c) for c in range(CHUNKS)]
+        raw = {}
         grouped = {}
-        queue = [("x", 0), ("proj", 0), ("proj", 1), ("x", 1)] + [("w", c) for c in range(N_CHUNKS)]
 
         def load_next():
-            if not queue:
+            if not to_load:
                 return
-            unit = queue.pop(0)
-            kind, idx = unit
-            t = raw.tile([P, 4096], BF16, name="rawt", tag="raw")
+            kind, idx = to_load.pop(0)
+            dest = raw_pool.tile([P, LOAD], BF16, name="raw", tag="raw")
             if kind == "proj":
-                nc.sync.dma_start(out=t[:].rearrange("p (a f) -> p a f", a=4), in_=proj_rows[:, 4 * idx:4 * idx + 4, :])
+                nc.sync.dma_start(out=dest[:].rearrange("p (a f) -> p a f", a=4), in_=proj_rows[:, 4 * idx:4 * idx + 4, :])
             elif kind == "x":
-                pieces = X_SPLIT if idx == 0 else 1
-                w = H // pieces
-                for q in range(pieces):
-                    nc.sync.dma_start(out=t[:].rearrange("p (i k) -> p i k", i=2)[:, :, w * q:w * (q + 1)],
-                                      in_=x_rows[:, 2 * idx:2 * idx + 2, w * q:w * (q + 1)])
+                nc.sync.dma_start(out=dest[:].rearrange("p (i k) -> p i k", i=2), in_=x_rows[:, 2 * idx:2 * idx + 2, :])
             else:
-                nc.sync.dma_start(out=t[:].rearrange("p (j n) -> p j n", j=4), in_=w_rows[:, :, W_CHUNK * idx:W_CHUNK * (idx + 1)])
-            loaded[unit] = t
+                nc.sync.dma_start(out=dest[:].rearrange("p (t n) -> p t n", t=PACK),
+                                  in_=w_rows[:, :, WORDS * idx:WORDS * (idx + 1)])
+            raw[(kind, idx)] = dest
 
-        urgent = []
-        pending = []
+        def new_grouped(kind, idx):
+            grouped[(kind, idx)] = grouped_pool.tile([P, LOAD], BF16, name="grouped", tag="grouped", align_bytes=64)
 
-        def tick():
-            if urgent:
-                urgent.pop(0)()
-            elif pending:
-                pending.pop(0)()
+        soon = []
+        later = []
 
-        def new_grouped(unit):
-            grouped[unit] = grp.tile([P, 4096], BF16, name="grpt", tag="grp", align_bytes=64)
+        def one_small_operation():
+            if soon:
+                soon.pop(0)()
+            elif later:
+                later.pop(0)()
 
-        def proj_regroup(idx):
-            unit = ("proj", idx)
-            new_grouped(unit)
-            for gl in range(2):
-                sl = slice(2048 * gl, 2048 * (gl + 1))
-                regroup(nc.vector.tensor_copy, grouped[unit][:, sl], loaded[unit][:, sl], 0, PROJ_V_COLS)
-                regroup(nc.scalar.copy, grouped[unit][:, sl], loaded[unit][:, sl], PROJ_V_COLS, P0)
+        def quantise(kind, idx):
+            words, scales = operands[kind]
+            cols = slice(WORDS * idx, WORDS * (idx + 1))
+            nc.vector.quantize_mx(out=words[:, cols].bitcast(FP8X4), scales=scales[:, cols], in_=grouped[(kind, idx)][:])
+            one_small_operation()
 
-        def quantise(unit):
-            kind, idx = unit
-            codes, scales = {"proj": (pq, ps), "x": (xq, xs), "w": (wq, ws)}[kind]
-            cols = slice(1024 * idx, 1024 * (idx + 1))
-            nc.vector.quantize_mx(out=codes[:, cols].bitcast(FP8X4), scales=scales[:, cols], in_=grouped[unit][:])
-            tick()
+        x_banks = {}
 
-        xbanks = {}
-
-        def x_transpose(idx):
-            unit = ("x", idx)
-            new_grouped(unit)
-            words = loaded[unit][:].bitcast(F32)
-            banks = []
-            for gp in range(4):
-                bank = psum.tile([P, BANK], F32, name="bank", tag="ps")
+        def transpose_x(idx):
+            new_grouped("x", idx)
+            pairs = raw[("x", idx)][:].bitcast(F32)
+            x_banks[idx] = []
+            for j in range(PASSES):
+                bank = psum.tile([P, BANK], F32, name="bank", tag="bank")
                 for u in range(2):
                     for i in range(2):
-                        src0 = 1024 * i + 256 * gp + 128 * u
-                        nc.tensor.transpose(out=bank[:, 256 * u + 128 * i:256 * u + 128 * (i + 1)],
-                                            in_=words[:, src0:src0 + 128], identity=ident[:])
-                banks.append(bank)
-            xbanks[idx] = banks
+                        first = H // 2 * i + PASS_PAIRS * j + P * u
+                        nc.tensor.transpose(out=bank[:, LOAD_TOKENS * u + P * i:LOAD_TOKENS * u + P * (i + 1)],
+                                            in_=pairs[:, first:first + P], identity=identity[:])
+                x_banks[idx].append(bank)
 
-        def x_copy(idx):
-            gwords = grouped[("x", idx)][:].bitcast(F32)
-            for gp in range(4):
-                copy = nc.vector.tensor_copy if gp >= 4 - X_V_BANKS else nc.scalar.copy
-                copy(out=gwords[:, 512 * gp:512 * (gp + 1)].rearrange("p (w u) -> p w u", u=2),
-                     in_=xbanks[idx][gp][:].rearrange("p (u w) -> p w u", u=2))
+        def copy_x(idx):
+            pairs = grouped[("x", idx)][:].bitcast(F32)
+            for j in range(PASSES):
+                copy = nc.vector.tensor_copy if j >= PASSES - X_VECTOR_BANKS else nc.scalar.copy
+                copy(out=pairs[:, BANK * j:BANK * (j + 1)].rearrange("p (m u) -> p m u", u=2),
+                     in_=x_banks[idx][j][:].rearrange("p (u m) -> p m u", u=2))
 
-        hbank = {}
-        hgrouped = {}
+        def regroup_proj(idx):
+            new_grouped("proj", idx)
+            for half in range(2):
+                part = slice(PACK * P0 * half, PACK * P0 * (half + 1))
+                dst, src = grouped[("proj", idx)][:, part], raw[("proj", idx)][:, part]
+                regroup(nc.vector.tensor_copy, dst, src, 0, PROJ_VECTOR_COLS)
+                regroup(nc.scalar.copy, dst, src, PROJ_VECTOR_COLS, P0)
 
-        def hidden_matmul(tt):
-            bank = psum.tile([P, BANK], F32, name="bank", tag="ps")
-            for j in range(4):
-                for gp in range(4):
-                    a = slice(512 * gp + 128 * j, 512 * gp + 128 * (j + 1))
-                    b0 = 1024 * (tt // 2) + 256 * gp + 128 * (tt % 2)
-                    b = slice(b0, b0 + 128)
-                    nc.tensor.matmul_mx(out=bank[:, 128 * j:128 * (j + 1)],
-                                        lhsT=pq[:, a].bitcast(FP8X4), lhsT_scale=ps[:, a],
-                                        rhs=xq[:, b].bitcast(FP8X4), rhs_scale=xs[:, b],
-                                        start=(gp == 0), stop=(gp == 3))
-            hbank[tt] = bank
+        h_bank = {}
+        h_grouped = {}
 
-        def hidden_copy(tt):
-            g = hgrp.tile([P, 512], BF16, name="hg", tag="hg", align_bytes=64)
-            nc.scalar.copy(out=g[:].rearrange("p (w j) -> p w j", j=4),
-                           in_=hbank[tt][:].rearrange("p (j w) -> p w j", j=4))
-            hgrouped[tt] = g
+        def multiply_h(tile):
+            bank = psum.tile([P, BANK], F32, name="bank", tag="bank")
+            for t in range(PACK):
+                for j in range(PASSES):
+                    proj_cols = slice(P0 * j + P * t, P0 * j + P * (t + 1))
+                    first = WORDS * (tile // 2) + LOAD_TOKENS * j + P * (tile % 2)
+                    tokens = slice(first, first + P)
+                    nc.tensor.matmul_mx(out=bank[:, P * t:P * (t + 1)],
+                                        lhsT=proj_words[:, proj_cols].bitcast(FP8X4), lhsT_scale=proj_scales[:, proj_cols],
+                                        rhs=x_words[:, tokens].bitcast(FP8X4), rhs_scale=x_scales[:, tokens],
+                                        start=(j == 0), stop=(j == PASSES - 1))
+            h_bank[tile] = bank
 
-        def hidden_quantise(tt):
-            cols = slice(128 * tt, 128 * (tt + 1))
-            nc.vector.quantize_mx(out=hq[:, cols].bitcast(FP8X4), scales=hs[:, cols], in_=hgrouped[tt][:])
+        def copy_h(tile):
+            h_grouped[tile] = h_pool.tile([P, PACK * P], BF16, name="h_grouped", tag="h_grouped", align_bytes=64)
+            nc.scalar.copy(out=h_grouped[tile][:].rearrange("p (m t) -> p m t", t=PACK),
+                           in_=h_bank[tile][:].rearrange("p (t m) -> p m t", t=PACK))
 
-        def w_regroup(idx):
-            unit = ("w", idx)
-            new_grouped(unit)
-            regroup(nc.vector.tensor_copy, grouped[unit][:], loaded[unit][:], 0, W_V_COLS[idx])
-            tick()
-            regroup(nc.scalar.copy, grouped[unit][:], loaded[unit][:], W_V_COLS[idx], W_CHUNK)
+        def quantise_h(tile):
+            tokens = slice(P * tile, P * (tile + 1))
+            nc.vector.quantize_mx(out=h_words[:, tokens].bitcast(FP8X4), scales=h_scales[:, tokens],
+                                  in_=h_grouped[tile][:])
 
-        state = {}
+        def regroup_w(c):
+            new_grouped("w", c)
+            regroup(nc.vector.tensor_copy, grouped[("w", c)][:], raw[("w", c)][:], 0, W_VECTOR_COLS[c])
+            one_small_operation()
+            regroup(nc.scalar.copy, grouped[("w", c)][:], raw[("w", c)][:], W_VECTOR_COLS[c], WORDS)
+
+        rows = {}
         exp_ready = []
 
-        def start_tile(tt):
-            state[tt] = {
-                "nm4": stat.tile([P, NG], F32, name="nm4", tag="nm4"),
-                "s16": stat.tile([P, 16], F32, name="s16", tag="s16"),
-                "e": {}, "gm": {}, "bank": {},
+        def start_tile(tile):
+            rows[tile] = {
+                "shift": row_pool.tile([P, GROUPS], F32, name="shift", tag="shift"),
+                "sums": row_pool.tile([P, BANKS], F32, name="sums", tag="sums"),
+                "numerators": {}, "maxima": {}, "bank": {},
             }
 
-        def logits(tt, b):
-            st = state[tt]
-            tcols = slice(128 * tt, 128 * (tt + 1))
-            bank = psum.tile([P, BANK], F32, name="bank", tag="ps")
-            n = slice(BANK * b, BANK * (b + 1))
-            nc.tensor.matmul_mx(out=bank[:], lhsT=hq[:, tcols].bitcast(FP8X4), lhsT_scale=hs[:, tcols],
-                                rhs=wq[:, n].bitcast(FP8X4), rhs_scale=ws[:, n], start=True, stop=True)
-            st["bank"][b] = bank
+        def multiply_logits(tile, b):
+            tokens = slice(P * tile, P * (tile + 1))
+            cols = slice(BANK * b, BANK * (b + 1))
+            bank = psum.tile([P, BANK], F32, name="bank", tag="bank")
+            nc.tensor.matmul_mx(out=bank[:], lhsT=h_words[:, tokens].bitcast(FP8X4), lhsT_scale=h_scales[:, tokens],
+                                rhs=w_words[:, cols].bitcast(FP8X4), rhs_scale=w_scales[:, cols], start=True, stop=True)
+            rows[tile]["bank"][b] = bank
 
-        def group_max(tt, g, now):
-            st = state[tt]
-            nc.vector.tensor_reduce(out=st["nm4"][:, g:g + 1], in_=st["gm"][g][:], axis=AX.X, op=ALU.max, negate=True)
-            for b in range(4 * g, 4 * g + 4):
-                exp_ready.append((tt, b))
-            if now and g < NG - 1:
-                run_exps(4)
+        def exponentials(count):
+            for ready in range(min(count, len(exp_ready))):
+                tile, b = exp_ready.pop(0)
+                row = rows[tile]
+                g = b // GROUP_BANKS
+                if b % GROUP_BANKS == 0:
+                    row["numerators"][g] = numerator_pool.tile([P, GROUP], F32, name="numerators", tag="numerators")
+                cols = slice(BANK * (b % GROUP_BANKS), BANK * (b % GROUP_BANKS + 1))
+                nc.scalar.activation(out=row["numerators"][g][:, cols], in_=row["bank"][b][:], func=AF.Exp,
+                                     bias=row["shift"][:, g:g + 1], scale=1.0, accum_out=row["sums"][:, b:b + 1])
 
-        def bank_max(tt, b, now):
-            st = state[tt]
-            g, i = b // 4, b % 4
-            if i == 0:
-                st["gm"][g] = gstat.tile([P, 4], F32, name="gm", tag="gm")
-            nc.vector.tensor_reduce(out=st["gm"][g][:, i:i + 1], in_=st["bank"][b][:], axis=AX.X, op=ALU.max)
-            tick()
-            if i == 3:
-                urgent.append(lambda: group_max(tt, g, now))
-                if g == NG - 1:
-                    urgent.append(lambda: fin_max(tt))
+        def group_shift(tile, g, at_once):
+            row = rows[tile]
+            nc.vector.tensor_reduce(out=row["shift"][:, g:g + 1], in_=row["maxima"][g][:], axis=AX.X, op=ALU.max,
+                                    negate=True)
+            exp_ready.extend([(tile, b) for b in range(GROUP_BANKS * g, GROUP_BANKS * (g + 1))])
+            if at_once and g < GROUPS - 1:
+                exponentials(GROUP_BANKS)
 
-        def run_exps(count):
-            for n in range(min(count, len(exp_ready))):
-                tt, b = exp_ready.pop(0)
-                st = state[tt]
-                g, i = b // 4, b % 4
-                if i == 0:
-                    st["e"][g] = epool.tile([P, GROUP], F32, name="e", tag="e")
-                nc.scalar.activation(out=st["e"][g][:, BANK * i:BANK * (i + 1)], in_=st["bank"][b][:], func=AF.Exp,
-                                     bias=st["nm4"][:, g:g + 1], scale=1.0, accum_out=st["s16"][:, b:b + 1])
+        def row_factors(tile):
+            row = rows[tile]
+            lowest = row_pool.tile([P, 1], F32, name="lowest", tag="lowest")
+            nc.vector.tensor_reduce(out=lowest[:], in_=row["shift"][:], axis=AX.X, op=ALU.min)
+            row["f"] = row_pool.tile([P, GROUPS], F32, name="f", tag="f")
+            nc.scalar.activation(out=row["f"][:], in_=row["shift"][:], func=AF.Exp, bias=lowest[:], scale=-1.0)
+            if tile > 0:
+                exponentials(GROUP_BANKS)
 
-        def fin_max(tt):
-            st = state[tt]
-            st["nmax"] = stat.tile([P, 1], F32, name="nmax", tag="nmax")
-            nc.vector.tensor_reduce(out=st["nmax"][:], in_=st["nm4"][:], axis=AX.X, op=ALU.min)
-            st["f4"] = stat.tile([P, NG], F32, name="f4", tag="f4")
-            nc.scalar.activation(out=st["f4"][:], in_=st["nm4"][:], func=AF.Exp, bias=st["nmax"][:], scale=-1.0)
-            if tt > 0:
-                run_exps(4)
+        def bank_maximum(tile, b, at_once):
+            row = rows[tile]
+            g = b // GROUP_BANKS
+            if b % GROUP_BANKS == 0:
+                row["maxima"][g] = maxima_pool.tile([P, GROUP_BANKS], F32, name="maxima", tag="maxima")
+            nc.vector.tensor_reduce(out=row["maxima"][g][:, b % GROUP_BANKS:b % GROUP_BANKS + 1], in_=row["bank"][b][:],
+                                    axis=AX.X, op=ALU.max)
+            one_small_operation()
+            if b % GROUP_BANKS == GROUP_BANKS - 1:
+                soon.append(lambda: group_shift(tile, g, at_once))
+                if g == GROUPS - 1:
+                    soon.append(lambda: row_factors(tile))
 
-        def fin_steps(tt, after):
-            st = state[tt]
-            junk = stat.tile([P, 4], F32, name="junk", tag="junk")
-            acc = stat.tile([P, NG], F32, name="acc", tag="acc")
-            rtot = stat.tile([P, 1], F32, name="rtot", tag="rtot")
-            st["sc4"] = stat.tile([P, NG], F32, name="sc4", tag="sc4")
+        def total_steps(tile, engine, then):
+            row = rows[tile]
+            products = row_pool.tile([P, GROUP_BANKS], F32, name="products", tag="products")
+            total = row_pool.tile([P, GROUPS], F32, name="total", tag="total")
+            inverse = row_pool.tile([P, 1], F32, name="inverse", tag="inverse")
+            row["factor"] = row_pool.tile([P, GROUPS], F32, name="factor", tag="factor")
 
             def add_group(g):
-                nc.vector.tensor_scalar(out=junk[:], in0=st["s16"][:, 4 * g:4 * g + 4], scalar1=st["f4"][:, g:g + 1],
-                                        scalar2=(acc[:, g - 1:g] if g else 0.0), op0=ALU.mult, op1=ALU.add,
-                                        accum_out=acc[:, g:g + 1])
+                nc.vector.tensor_scalar(out=products[:], in0=row["sums"][:, GROUP_BANKS * g:GROUP_BANKS * (g + 1)],
+                                        scalar1=row["f"][:, g:g + 1], scalar2=(total[:, g - 1:g] if g else 0.0),
+                                        op0=ALU.mult, op1=ALU.add, accum_out=total[:, g:g + 1])
 
-            def last():
-                nc.vector.reciprocal(out=rtot[:], in_=acc[:, NG - 1:NG])
-                FIN_ENGINE[tt].tensor_scalar(out=st["sc4"][:], in0=st["f4"][:], scalar1=rtot[:], scalar2=prob[:, tt:tt + 1],
-                                             op0=ALU.mult, op1=ALU.mult)
-                after()
+            def factors():
+                nc.vector.reciprocal(out=inverse[:], in_=total[:, GROUPS - 1:GROUPS])
+                engine.tensor_scalar(out=row["factor"][:], in0=row["f"][:], scalar1=inverse[:],
+                                     scalar2=prob[:, tile:tile + 1], op0=ALU.mult, op1=ALU.mult)
+                then()
 
-            return [lambda: add_group(0), lambda: add_group(1), lambda: add_group(2), lambda: add_group(3), last]
+            return [lambda: add_group(0), lambda: add_group(1), lambda: add_group(2), lambda: add_group(3), factors]
 
-        def scale_store(tt, g, engine, c0=0, c1=GROUP):
-            st = state[tt]
-            e = st["e"][g][:, c0:c1]
-            s = st["sc4"][:, g:g + 1]
-            if engine == "g":
-                nc.gpsimd.tensor_scalar(out=e, in0=e, scalar1=s, scalar2=0.0, op0=ALU.mult, op1=ALU.add)
-            elif engine == "v":
-                nc.vector.tensor_scalar(out=e, in0=e, scalar1=s, scalar2=None, op0=ALU.mult)
+        def scale_and_store(tile, g, engine):
+            numerators = rows[tile]["numerators"][g][:]
+            factor = rows[tile]["factor"][:, g:g + 1]
+            if engine == "gpsimd":
+                nc.gpsimd.tensor_scalar(out=numerators, in0=numerators, scalar1=factor, scalar2=0.0,
+                                        op0=ALU.mult, op1=ALU.add)
+            elif engine == "vector":
+                nc.vector.tensor_scalar(out=numerators, in0=numerators, scalar1=factor, scalar2=None, op0=ALU.mult)
             else:
-                nc.scalar.activation(out=e, in_=e, func=AF.Copy, scale=s)
-            nc.sync.dma_start(out=out_rows[128 * tt:128 * (tt + 1), GROUP * g + c0:GROUP * g + c1], in_=e)
+                nc.scalar.activation(out=numerators, in_=numerators, func=AF.Copy, scale=factor)
+            nc.sync.dma_start(out=out_rows[P * tile:P * (tile + 1), GROUP * g:GROUP * (g + 1)], in_=numerators)
 
-        FIN_ENGINE = [nc.gpsimd, nc.gpsimd, nc.gpsimd, nc.vector]
-        late = []
+        def gpsimd_share(tile):
+            for g in range(GPSIMD_GROUPS[tile]):
+                scale_and_store(tile, g, "gpsimd")
 
-        def gpsimd_scales(tt):
-            for g in range(NG):
-                if MID[tt][g] == "g":
-                    scale_store(tt, g, "g")
-                else:
-                    late.append((tt, g, MID[tt][g]))
-
-        for n in range(RAW_BUFS):
+        for ahead in range(LOADS_AHEAD):
             load_next()
-        x_transpose(0)
-        x_copy(0)
+        transpose_x(0)
+        copy_x(0)
         load_next()
-        proj_regroup(0)
+        regroup_proj(0)
         load_next()
-        quantise(("x", 0))
-        proj_regroup(1)
+        quantise("x", 0)
+        regroup_proj(1)
         load_next()
-        quantise(("proj", 0))
-        x_transpose(1)
-        quantise(("proj", 1))
-        hidden_matmul(0)
-        hidden_matmul(1)
-        x_copy(1)
+        quantise("proj", 0)
+        transpose_x(1)
+        quantise("proj", 1)
+        multiply_h(0)
+        multiply_h(1)
+        copy_x(1)
         load_next()
 
         start_tile(0)
-        for c in range(N_CHUNKS + M_LAG):
-            if 1 <= c <= N_CHUNKS:
-                quantise(("w", c - 1))
-                logits(0, 2 * (c - 1))
-                logits(0, 2 * (c - 1) + 1)
-            if c < N_CHUNKS:
-                w_regroup(c)
+        for c in range(CHUNKS + MAX_LAG):
+            if 1 <= c <= CHUNKS:
+                quantise("w", c - 1)
+                for b in range(CHUNK_BANKS * (c - 1), CHUNK_BANKS * c):
+                    multiply_logits(0, b)
+            if c < CHUNKS:
+                regroup_w(c)
                 load_next()
             if c == 0:
-                quantise(("x", 1))
-                hidden_copy(0)
-                hidden_copy(1)
-                hidden_matmul(2)
-                hidden_matmul(3)
-                hidden_quantise(0)
+                quantise("x", 1)
+                copy_h(0)
+                copy_h(1)
+                multiply_h(2)
+                multiply_h(3)
+                quantise_h(0)
             if c == 1:
-                hidden_copy(2)
-                hidden_copy(3)
-                hidden_quantise(1)
+                copy_h(2)
+                copy_h(3)
+                quantise_h(1)
             if c == 2:
-                hidden_quantise(2)
-                hidden_quantise(3)
-            if c == N_CHUNKS - 1:
-                with nc.allow_non_contiguous_dma(reason="512 two-byte values, one column per token tile"):
-                    nc.sync.dma_start(out=prob_bf[:], in_=prob_cols)
-            if c == N_CHUNKS + 1:
-                nc.vector.tensor_copy(out=prob[:], in_=prob_bf[:])
-            run_exps(2)
-            d = c - M_LAG
-            if d >= 0:
-                bank_max(0, 2 * d, False)
-                bank_max(0, 2 * d + 1, False)
+                quantise_h(2)
+                quantise_h(3)
+            if c == CHUNKS - 1:
+                with nc.allow_non_contiguous_dma(reason="512 two-byte values, one column for each token tile"):
+                    nc.sync.dma_start(out=prob_bf16[:], in_=prob_cols)
+            if c == CHUNKS + 1:
+                nc.vector.tensor_copy(out=prob[:], in_=prob_bf16[:])
+            exponentials(CHUNK_BANKS)
+            if c >= MAX_LAG:
+                for b in range(CHUNK_BANKS * (c - MAX_LAG), CHUNK_BANKS * (c - MAX_LAG + 1)):
+                    bank_maximum(0, b, False)
 
-        for tt in range(1, 4):
-            start_tile(tt)
-            for b in range(16):
-                if b % 4 == 0:
-                    for i in range(4):
-                        logits(tt, b + i)
-                bank_max(tt, b, True)
-                if tt == 1 and b < 2:
-                    run_exps(4)
-                if b == FIN_LAG:
-                    pending.extend(fin_steps(tt - 1, lambda: gpsimd_scales(tt - 1)))
-        while urgent or pending:
-            tick()
-        for tt, g, engine in late:
-            scale_store(tt, g, {"v": "v", "G": "g", "s": "s"}[engine])
+        for tile in range(1, TILES):
+            start_tile(tile)
+            for b in range(BANKS):
+                if b % GROUP_BANKS == 0:
+                    for ahead in range(GROUP_BANKS):
+                        multiply_logits(tile, b + ahead)
+                bank_maximum(tile, b, True)
+                if tile == 1 and b < 2:
+                    exponentials(GROUP_BANKS)
+                if b == TOTAL_BEHIND_BANK[tile - 1]:
+                    later.extend(total_steps(tile - 1, nc.gpsimd, lambda: gpsimd_share(tile - 1)))
+        while soon or later:
+            one_small_operation()
 
-        def tail():
-            for g, engine, c0, c1 in TAIL:
-                scale_store(3, g, engine, c0, c1)
+        for g in range(GPSIMD_GROUPS[TILES - 2], GROUPS):
+            scale_and_store(TILES - 2, g, "vector")
 
-        for step in fin_steps(3, tail):
-            step()
+        def last_tile():
+            for g, engine in enumerate(["vector", "scalar", "vector", "vector"]):
+                scale_and_store(TILES - 1, g, engine)
+
+        for operation in total_steps(TILES - 1, nc.vector, last_tile):
+            operation()

@@ -25,9 +25,9 @@ PASS_PAIRS = P * PACK // 2
 TILES = TOKENS // P
 BANK = 512
 BANKS = V0 // BANK
-GROUP_BANKS = 4
-GROUP = GROUP_BANKS * BANK
-GROUPS = V0 // GROUP
+GROUP_BANKS = [2, 4, 4, 4]
+MOST_GROUPS = BANKS // min(GROUP_BANKS)
+WIDEST_GROUP = max(GROUP_BANKS) * BANK
 LOAD = 4096
 WORDS = LOAD // PACK
 LOAD_TOKENS = LOAD // H * P
@@ -37,11 +37,14 @@ RUN = 4
 
 LOADS_AHEAD = 5
 PROJ_VECTOR_COLS = 256
-W_VECTOR_COLS = [576, 576] + [416] * (CHUNKS - 2)
+W_VECTOR_COLS = [576, 432] + [336] * (CHUNKS - 2)
+TENSOR_COLS = [0] + [512] * (CHUNKS - 1)
+SPREAD_COLS = 128
+SPREAD_BANK_COLS = 256
 X_VECTOR_BANKS = 1
-MAX_LAG = 2
-TOTAL_BEHIND_BANK = [4, 1, 1]
-GPSIMD_GROUPS = [4, 4, 1]
+LOGITS_LAG = 2
+TOTAL_BEHIND_BANK = [0, 1, 1]
+GPSIMD_GROUPS = [8, 4, 2]
 
 
 def regroup(copy, dst, src, first, last):
@@ -63,14 +66,16 @@ def tile_adaptiveinputsoftmax_pa_kernel(tc, x, tail_proj_0, tail_w_0, cluster_pr
         raw_pool = ctx.enter_context(tc.tile_pool(name="raw", bufs=LOADS_AHEAD))
         grouped_pool = ctx.enter_context(tc.tile_pool(name="grouped", bufs=3))
         h_pool = ctx.enter_context(tc.tile_pool(name="h", bufs=2))
-        numerator_pool = ctx.enter_context(tc.tile_pool(name="numerators", bufs=3 * GROUPS))
+        numerator_pool = ctx.enter_context(tc.tile_pool(name="numerators", bufs=12))
         row_pool = ctx.enter_context(tc.tile_pool(name="row", bufs=TILES))
-        maxima_pool = ctx.enter_context(tc.tile_pool(name="maxima", bufs=GROUPS))
-        psum = ctx.enter_context(tc.psum_pool(name="psum", bufs=8))
+        psum = ctx.enter_context(tc.psum_pool(name="psum", bufs=6))
+        psum_spread = ctx.enter_context(tc.psum_pool(name="psum_spread", bufs=2))
         ctx.enter_context(tc.manual_schedule())
 
         identity = keep.tile([P, P], F32, name="identity")
         make_identity(nc, identity[:])
+        identity_bf16 = keep.tile([P, P], BF16, name="identity_bf16")
+        make_identity(nc, identity_bf16[:])
         zero = keep.tile([P, 1], F32, name="zero")
         nc.vector.memset(zero[:], 0.0)
         one = keep.tile([P, 1], F32, name="one")
@@ -115,7 +120,7 @@ def tile_adaptiveinputsoftmax_pa_kernel(tc, x, tail_proj_0, tail_w_0, cluster_pr
         def one_small_operation():
             if soon:
                 soon.pop(0)()
-            elif later:
+            if later:
                 later.pop(0)()
 
         def quantise(kind, idx):
@@ -158,7 +163,10 @@ def tile_adaptiveinputsoftmax_pa_kernel(tc, x, tail_proj_0, tail_w_0, cluster_pr
         h_grouped = {}
 
         def multiply_h(tile):
-            bank = psum.tile([P, BANK], F32, name="bank", tag="bank")
+            if tile < 2:
+                bank = psum.tile([P, BANK], F32, name="bank", tag="bank")
+            else:
+                bank = psum_spread.tile([P, BANK], F32, name="spread", tag="spread")
             for t in range(PACK):
                 for j in range(PASSES):
                     proj_cols = slice(P0 * j + P * t, P0 * j + P * (t + 1))
@@ -180,26 +188,48 @@ def tile_adaptiveinputsoftmax_pa_kernel(tc, x, tail_proj_0, tail_w_0, cluster_pr
             nc.vector.quantize_mx(out=h_words[:, tokens].bitcast(FP8X4), scales=h_scales[:, tokens],
                                   in_=h_grouped[tile][:])
 
+        spread = {}
+
+        def spread_w(c, which):
+            by_column = raw[("w", c)][:].rearrange("p (t n) -> p n t", t=PACK)
+            for first in [WORDS - TENSOR_COLS[c] + SPREAD_BANK_COLS * which]:
+                bank = psum_spread.tile([P, PACK * SPREAD_BANK_COLS], BF16, name="spread", tag="spread")
+                for part in range(SPREAD_BANK_COLS // SPREAD_COLS):
+                    cols = slice(first + SPREAD_COLS * part, first + SPREAD_COLS * (part + 1))
+                    side_by_side = bank[:, PACK * SPREAD_COLS * part:PACK * SPREAD_COLS * (part + 1)]
+                    nc.tensor.matmul(out=side_by_side.rearrange("p (n t) -> p n t", t=PACK), lhsT=identity_bf16[:],
+                                     rhs=by_column[:, cols, :], start=True, stop=True)
+                spread.setdefault(c, []).append((first, bank))
+
         def regroup_w(c):
             new_grouped("w", c)
             regroup(nc.vector.tensor_copy, grouped[("w", c)][:], raw[("w", c)][:], 0, W_VECTOR_COLS[c])
             one_small_operation()
-            regroup(nc.scalar.copy, grouped[("w", c)][:], raw[("w", c)][:], W_VECTOR_COLS[c], WORDS)
+            for first, bank in spread.get(c, []):
+                nc.scalar.copy(out=grouped[("w", c)][:, PACK * first:PACK * (first + SPREAD_BANK_COLS)], in_=bank[:])
+            regroup(nc.scalar.copy, grouped[("w", c)][:], raw[("w", c)][:], W_VECTOR_COLS[c], WORDS - TENSOR_COLS[c])
 
         rows = {}
         exp_ready = []
 
+        def groups_of(tile):
+            return BANKS // GROUP_BANKS[tile]
+
         def start_tile(tile):
             rows[tile] = {
-                "shift": row_pool.tile([P, GROUPS], F32, name="shift", tag="shift"),
+                "shift": row_pool.tile([P, MOST_GROUPS], F32, name="shift", tag="shift"),
                 "sums": row_pool.tile([P, BANKS], F32, name="sums", tag="sums"),
-                "numerators": {}, "maxima": {}, "bank": {},
+                "maxima": row_pool.tile([P, BANKS], F32, name="maxima", tag="maxima"),
+                "numerators": {}, "bank": {},
             }
 
         def multiply_logits(tile, b):
             tokens = slice(P * tile, P * (tile + 1))
             cols = slice(BANK * b, BANK * (b + 1))
-            bank = psum.tile([P, BANK], F32, name="bank", tag="bank")
+            if tile > 0 and b % 4 == 0:
+                bank = psum_spread.tile([P, BANK], F32, name="spread", tag="spread")
+            else:
+                bank = psum.tile([P, BANK], F32, name="bank", tag="bank")
             nc.tensor.matmul_mx(out=bank[:], lhsT=h_words[:, tokens].bitcast(FP8X4), lhsT_scale=h_scales[:, tokens],
                                 rhs=w_words[:, cols].bitcast(FP8X4), rhs_scale=w_scales[:, cols], start=True, stop=True)
             rows[tile]["bank"][b] = bank
@@ -208,66 +238,79 @@ def tile_adaptiveinputsoftmax_pa_kernel(tc, x, tail_proj_0, tail_w_0, cluster_pr
             for ready in range(min(count, len(exp_ready))):
                 tile, b = exp_ready.pop(0)
                 row = rows[tile]
-                g = b // GROUP_BANKS
-                if b % GROUP_BANKS == 0:
-                    row["numerators"][g] = numerator_pool.tile([P, GROUP], F32, name="numerators", tag="numerators")
-                cols = slice(BANK * (b % GROUP_BANKS), BANK * (b % GROUP_BANKS + 1))
-                nc.scalar.activation(out=row["numerators"][g][:, cols], in_=row["bank"][b][:], func=AF.Exp,
-                                     bias=row["shift"][:, g:g + 1], scale=1.0, accum_out=row["sums"][:, b:b + 1])
+                g, place = divmod(b, GROUP_BANKS[tile])
+                if place == 0:
+                    row["numerators"][g] = numerator_pool.tile([P, BANK * GROUP_BANKS[tile]], F32, name="numerators",
+                                                               tag="numerators")
+                nc.scalar.activation(out=row["numerators"][g][:, BANK * place:BANK * (place + 1)], in_=row["bank"][b][:],
+                                     func=AF.Exp, bias=row["shift"][:, g:g + 1], scale=1.0,
+                                     accum_out=row["sums"][:, b:b + 1])
 
         def group_shift(tile, g, at_once):
             row = rows[tile]
-            nc.vector.tensor_reduce(out=row["shift"][:, g:g + 1], in_=row["maxima"][g][:], axis=AX.X, op=ALU.max,
-                                    negate=True)
-            exp_ready.extend([(tile, b) for b in range(GROUP_BANKS * g, GROUP_BANKS * (g + 1))])
-            if at_once and g < GROUPS - 1:
-                exponentials(GROUP_BANKS)
-
-        def row_factors(tile):
-            row = rows[tile]
-            lowest = row_pool.tile([P, 1], F32, name="lowest", tag="lowest")
-            nc.vector.tensor_reduce(out=lowest[:], in_=row["shift"][:], axis=AX.X, op=ALU.min)
-            row["f"] = row_pool.tile([P, GROUPS], F32, name="f", tag="f")
-            nc.scalar.activation(out=row["f"][:], in_=row["shift"][:], func=AF.Exp, bias=lowest[:], scale=-1.0)
-            if tile > 0:
-                exponentials(GROUP_BANKS)
+            count = groups_of(tile)
+            nc.vector.tensor_reduce(out=row["shift"][:, g:g + 1], in_=row["maxima"][:, 0:GROUP_BANKS[tile] * (g + 1)],
+                                    axis=AX.X, op=ALU.max, negate=True)
+            exp_ready.extend([(tile, b) for b in range(GROUP_BANKS[tile] * g, GROUP_BANKS[tile] * (g + 1))])
+            if g == count - 1:
+                row["f"] = row_pool.tile([P, MOST_GROUPS], F32, name="f", tag="f")
+                nc.scalar.activation(out=row["f"][:, 0:count], in_=row["shift"][:, 0:count], func=AF.Exp,
+                                     bias=row["shift"][:, count - 1:count], scale=-1.0)
+            if at_once:
+                exponentials(GROUP_BANKS[tile])
 
         def bank_maximum(tile, b, at_once):
             row = rows[tile]
-            g = b // GROUP_BANKS
-            if b % GROUP_BANKS == 0:
-                row["maxima"][g] = maxima_pool.tile([P, GROUP_BANKS], F32, name="maxima", tag="maxima")
-            nc.vector.tensor_reduce(out=row["maxima"][g][:, b % GROUP_BANKS:b % GROUP_BANKS + 1], in_=row["bank"][b][:],
-                                    axis=AX.X, op=ALU.max)
+            g, place = divmod(b, GROUP_BANKS[tile])
+            nc.vector.tensor_reduce(out=row["maxima"][:, b:b + 1], in_=row["bank"][b][:], axis=AX.X, op=ALU.max)
             one_small_operation()
-            if b % GROUP_BANKS == GROUP_BANKS - 1:
+            if place == GROUP_BANKS[tile] - 1:
                 soon.append(lambda: group_shift(tile, g, at_once))
-                if g == GROUPS - 1:
-                    soon.append(lambda: row_factors(tile))
 
-        def total_steps(tile, engine, then):
+        def total_steps(tile, engine, then, at_a_stroke=False):
             row = rows[tile]
-            products = row_pool.tile([P, GROUP_BANKS], F32, name="products", tag="products")
-            total = row_pool.tile([P, GROUPS], F32, name="total", tag="total")
+            width = GROUP_BANKS[tile]
+            products = row_pool.tile([P, max(GROUP_BANKS)], F32, name="products", tag="products")
+            total = row_pool.tile([P, MOST_GROUPS], F32, name="total", tag="total")
             inverse = row_pool.tile([P, 1], F32, name="inverse", tag="inverse")
-            row["factor"] = row_pool.tile([P, GROUPS], F32, name="factor", tag="factor")
+            row["factor"] = row_pool.tile([P, MOST_GROUPS], F32, name="factor", tag="factor")
+
+            count = groups_of(tile)
 
             def add_group(g):
-                nc.vector.tensor_scalar(out=products[:], in0=row["sums"][:, GROUP_BANKS * g:GROUP_BANKS * (g + 1)],
+                nc.vector.tensor_scalar(out=products[:, 0:width], in0=row["sums"][:, width * g:width * (g + 1)],
                                         scalar1=row["f"][:, g:g + 1], scalar2=(total[:, g - 1:g] if g else 0.0),
                                         op0=ALU.mult, op1=ALU.add, accum_out=total[:, g:g + 1])
 
+            def group_sums():
+                nc.vector.tensor_reduce(out=sums_by_group[:, 0:count - 1],
+                                        in_=row["sums"][:, 0:width * (count - 1)].rearrange("p (g b) -> p g b", b=width),
+                                        axis=AX.X, op=ALU.add)
+
+            def weigh_groups():
+                nc.vector.scalar_tensor_tensor(out=weighted[:, 0:count - 1], in0=sums_by_group[:, 0:count - 1], scalar=1.0,
+                                               in1=row["f"][:, 0:count - 1], op0=ALU.mult, op1=ALU.mult,
+                                               accum_out=total[:, count - 2:count - 1])
+
             def factors():
-                nc.vector.reciprocal(out=inverse[:], in_=total[:, GROUPS - 1:GROUPS])
-                engine.tensor_scalar(out=row["factor"][:], in0=row["f"][:], scalar1=inverse[:],
-                                     scalar2=prob[:, tile:tile + 1], op0=ALU.mult, op1=ALU.mult)
+                nc.vector.reciprocal(out=inverse[:], in_=total[:, count - 1:count])
+                engine.tensor_scalar(out=row["factor"][:, 0:count], in0=row["f"][:, 0:count],
+                                     scalar1=inverse[:], scalar2=prob[:, tile:tile + 1], op0=ALU.mult, op1=ALU.mult)
                 then()
 
-            return [lambda: add_group(0), lambda: add_group(1), lambda: add_group(2), lambda: add_group(3), factors]
+            def adder(g):
+                return lambda: add_group(g)
+
+            if at_a_stroke:
+                sums_by_group = row_pool.tile([P, MOST_GROUPS], F32, name="sums_by_group", tag="sums_by_group")
+                weighted = row_pool.tile([P, MOST_GROUPS], F32, name="weighted", tag="weighted")
+                return [group_sums, weigh_groups, adder(count - 1), factors]
+            return [adder(g) for g in range(count)] + [factors]
 
         def scale_and_store(tile, g, engine):
             numerators = rows[tile]["numerators"][g][:]
             factor = rows[tile]["factor"][:, g:g + 1]
+            width = BANK * GROUP_BANKS[tile]
             if engine == "gpsimd":
                 nc.gpsimd.tensor_scalar(out=numerators, in0=numerators, scalar1=factor, scalar2=0.0,
                                         op0=ALU.mult, op1=ALU.add)
@@ -275,7 +318,7 @@ def tile_adaptiveinputsoftmax_pa_kernel(tc, x, tail_proj_0, tail_w_0, cluster_pr
                 nc.vector.tensor_scalar(out=numerators, in0=numerators, scalar1=factor, scalar2=None, op0=ALU.mult)
             else:
                 nc.scalar.activation(out=numerators, in_=numerators, func=AF.Copy, scale=factor)
-            nc.sync.dma_start(out=out_rows[P * tile:P * (tile + 1), GROUP * g:GROUP * (g + 1)], in_=numerators)
+            nc.sync.dma_start(out=out_rows[P * tile:P * (tile + 1), width * g:width * (g + 1)], in_=numerators)
 
         def gpsimd_share(tile):
             for g in range(GPSIMD_GROUPS[tile]):
@@ -300,26 +343,33 @@ def tile_adaptiveinputsoftmax_pa_kernel(tc, x, tail_proj_0, tail_w_0, cluster_pr
         load_next()
 
         start_tile(0)
-        for c in range(CHUNKS + MAX_LAG):
+        for c in range(CHUNKS + LOGITS_LAG + 1):
             if 1 <= c <= CHUNKS:
                 quantise("w", c - 1)
-                for b in range(CHUNK_BANKS * (c - 1), CHUNK_BANKS * c):
-                    multiply_logits(0, b)
             if c < CHUNKS:
                 regroup_w(c)
                 load_next()
+            if c + 1 < CHUNKS:
+                spread_w(c + 1, 0)
+            if 0 <= c - LOGITS_LAG < CHUNKS:
+                for b in range(CHUNK_BANKS * (c - LOGITS_LAG), CHUNK_BANKS * (c - LOGITS_LAG + 1)):
+                    multiply_logits(0, b)
+            if c + 1 < CHUNKS:
+                spread_w(c + 1, 1)
             if c == 0:
                 quantise("x", 1)
                 copy_h(0)
                 copy_h(1)
-                multiply_h(2)
-                multiply_h(3)
                 quantise_h(0)
             if c == 1:
+                quantise_h(1)
+            if c == CHUNKS:
+                multiply_h(2)
+                multiply_h(3)
+            if c == CHUNKS + 1:
                 copy_h(2)
                 copy_h(3)
-                quantise_h(1)
-            if c == 2:
+            if c == CHUNKS + 2:
                 quantise_h(2)
                 quantise_h(3)
             if c == CHUNKS - 1:
@@ -328,25 +378,23 @@ def tile_adaptiveinputsoftmax_pa_kernel(tc, x, tail_proj_0, tail_w_0, cluster_pr
             if c == CHUNKS + 1:
                 nc.vector.tensor_copy(out=prob[:], in_=prob_bf16[:])
             exponentials(CHUNK_BANKS)
-            if c >= MAX_LAG:
-                for b in range(CHUNK_BANKS * (c - MAX_LAG), CHUNK_BANKS * (c - MAX_LAG + 1)):
-                    bank_maximum(0, b, False)
+            if c >= LOGITS_LAG + 1:
+                for b in range(CHUNK_BANKS * (c - LOGITS_LAG - 1), CHUNK_BANKS * (c - LOGITS_LAG)):
+                    bank_maximum(0, b, c >= CHUNKS)
 
         for tile in range(1, TILES):
             start_tile(tile)
             for b in range(BANKS):
-                if b % GROUP_BANKS == 0:
-                    for ahead in range(GROUP_BANKS):
+                if b % GROUP_BANKS[tile] == 0:
+                    for ahead in range(GROUP_BANKS[tile]):
                         multiply_logits(tile, b + ahead)
                 bank_maximum(tile, b, True)
-                if tile == 1 and b < 2:
-                    exponentials(GROUP_BANKS)
                 if b == TOTAL_BEHIND_BANK[tile - 1]:
-                    later.extend(total_steps(tile - 1, nc.gpsimd, lambda: gpsimd_share(tile - 1)))
+                    later.extend(total_steps(tile - 1, nc.gpsimd, lambda: gpsimd_share(tile - 1), tile == 1))
         while soon or later:
             one_small_operation()
 
-        for g in range(GPSIMD_GROUPS[TILES - 2], GROUPS):
+        for g in range(GPSIMD_GROUPS[TILES - 2], groups_of(TILES - 2)):
             scale_and_store(TILES - 2, g, "vector")
 
         def last_tile():

@@ -25,7 +25,7 @@ PASS_PAIRS = P * PACK // 2
 TILES = TOKENS // P
 BANK = 512
 BANKS = V0 // BANK
-GROUP_BANKS = [2, 4, 4, 4]
+GROUP_BANKS = [4, 4, 4, 4]
 MOST_GROUPS = BANKS // min(GROUP_BANKS)
 WIDEST_GROUP = max(GROUP_BANKS) * BANK
 LOAD = 4096
@@ -37,14 +37,15 @@ RUN = 4
 
 LOADS_AHEAD = 5
 PROJ_VECTOR_COLS = 256
-W_VECTOR_COLS = [576, 432] + [336] * (CHUNKS - 2)
-TENSOR_COLS = [0] + [512] * (CHUNKS - 1)
+W_VECTOR_COLS = [576, 576, 416, 416, 416, 416, 416, 416]
+TENSOR_COLS = [0, 0, 0, 0, 0, 0, 0, 0]
 SPREAD_COLS = 128
 SPREAD_BANK_COLS = 256
 X_VECTOR_BANKS = 1
-LOGITS_LAG = 2
+LOGITS_LAG = 1
+H_STEP = 0
 TOTAL_BEHIND_BANK = [0, 1, 1]
-GPSIMD_GROUPS = [8, 4, 2]
+GPSIMD_GROUPS = [BANKS // GROUP_BANKS[0], 4, 2]
 
 
 def regroup(copy, dst, src, first, last):
@@ -163,7 +164,7 @@ def tile_adaptiveinputsoftmax_pa_kernel(tc, x, tail_proj_0, tail_w_0, cluster_pr
         h_grouped = {}
 
         def multiply_h(tile):
-            if tile < 2:
+            if tile < 2 or H_STEP == 0:
                 bank = psum.tile([P, BANK], F32, name="bank", tag="bank")
             else:
                 bank = psum_spread.tile([P, BANK], F32, name="spread", tag="spread")
@@ -193,8 +194,10 @@ def tile_adaptiveinputsoftmax_pa_kernel(tc, x, tail_proj_0, tail_w_0, cluster_pr
         def spread_w(c, which):
             by_column = raw[("w", c)][:].rearrange("p (t n) -> p n t", t=PACK)
             for first in [WORDS - TENSOR_COLS[c] + SPREAD_BANK_COLS * which]:
+                if first >= WORDS:
+                    continue
                 bank = psum_spread.tile([P, PACK * SPREAD_BANK_COLS], BF16, name="spread", tag="spread")
-                for part in range(SPREAD_BANK_COLS // SPREAD_COLS):
+                for part in range(min(SPREAD_BANK_COLS, WORDS - first) // SPREAD_COLS):
                     cols = slice(first + SPREAD_COLS * part, first + SPREAD_COLS * (part + 1))
                     side_by_side = bank[:, PACK * SPREAD_COLS * part:PACK * SPREAD_COLS * (part + 1)]
                     nc.tensor.matmul(out=side_by_side.rearrange("p (n t) -> p n t", t=PACK), lhsT=identity_bf16[:],
@@ -206,7 +209,8 @@ def tile_adaptiveinputsoftmax_pa_kernel(tc, x, tail_proj_0, tail_w_0, cluster_pr
             regroup(nc.vector.tensor_copy, grouped[("w", c)][:], raw[("w", c)][:], 0, W_VECTOR_COLS[c])
             one_small_operation()
             for first, bank in spread.get(c, []):
-                nc.scalar.copy(out=grouped[("w", c)][:, PACK * first:PACK * (first + SPREAD_BANK_COLS)], in_=bank[:])
+                cols = min(SPREAD_BANK_COLS, WORDS - first)
+                nc.scalar.copy(out=grouped[("w", c)][:, PACK * first:PACK * (first + cols)], in_=bank[:, 0:PACK * cols])
             regroup(nc.scalar.copy, grouped[("w", c)][:], raw[("w", c)][:], W_VECTOR_COLS[c], WORDS - TENSOR_COLS[c])
 
         rows = {}
@@ -226,7 +230,7 @@ def tile_adaptiveinputsoftmax_pa_kernel(tc, x, tail_proj_0, tail_w_0, cluster_pr
         def multiply_logits(tile, b):
             tokens = slice(P * tile, P * (tile + 1))
             cols = slice(BANK * b, BANK * (b + 1))
-            if tile > 0 and b % 4 == 0:
+            if (tile > 0 or sum(TENSOR_COLS) == 0) and b % 4 == 0:
                 bank = psum_spread.tile([P, BANK], F32, name="spread", tag="spread")
             else:
                 bank = psum.tile([P, BANK], F32, name="bank", tag="bank")
@@ -360,16 +364,17 @@ def tile_adaptiveinputsoftmax_pa_kernel(tc, x, tail_proj_0, tail_w_0, cluster_pr
                 quantise("x", 1)
                 copy_h(0)
                 copy_h(1)
-                quantise_h(0)
-            if c == 1:
-                quantise_h(1)
-            if c == CHUNKS:
+            if c == H_STEP:
                 multiply_h(2)
                 multiply_h(3)
-            if c == CHUNKS + 1:
+            if c == 0:
+                quantise_h(0)
+            if c == H_STEP + 1:
                 copy_h(2)
                 copy_h(3)
-            if c == CHUNKS + 2:
+            if c == 1:
+                quantise_h(1)
+            if c == H_STEP + 2:
                 quantise_h(2)
                 quantise_h(3)
             if c == CHUNKS - 1:

@@ -37,12 +37,15 @@ RUN = 4
 
 LOADS_AHEAD = 5
 PROJ_VECTOR_COLS = 256
-W_VECTOR_COLS = [576, 576, 416, 416, 416, 416, 416, 416]
+W_VECTOR_COLS = [576, 576, 320, 320, 320, 320, 320, 320]
 TENSOR_COLS = [0, 0, 0, 0, 0, 0, 0, 0]
 SPREAD_COLS = 128
 SPREAD_BANK_COLS = 256
+W_GPSIMD_COLS = [0, 0, 160, 160, 160, 160, 160, 160]
 X_VECTOR_BANKS = 1
 LOGITS_LAG = 1
+OVERLAP = 0
+HEAD = 0
 H_STEP = 0
 TOTAL_BEHIND_BANK = [0, 1, 1]
 GPSIMD_GROUPS = [BANKS // GROUP_BANKS[0], 4, 2]
@@ -94,7 +97,7 @@ def tile_adaptiveinputsoftmax_pa_kernel(tc, x, tail_proj_0, tail_w_0, cluster_pr
         prob_bf16 = keep.tile([P, TILES], BF16, name="prob_bf16")
         prob = keep.tile([P, TILES], F32, name="prob")
 
-        to_load = [("x", 0), ("proj", 0), ("proj", 1), ("x", 1)] + [("w", c) for c in range(CHUNKS)]
+        to_load = ([("proj", 0), ("x", 0), ("proj", 1), ("x", 1)] if HEAD == 1 else [("x", 0), ("proj", 0), ("proj", 1), ("x", 1)]) + [("w", c) for c in range(CHUNKS)]
         raw = {}
         grouped = {}
 
@@ -103,7 +106,11 @@ def tile_adaptiveinputsoftmax_pa_kernel(tc, x, tail_proj_0, tail_w_0, cluster_pr
                 return
             kind, idx = to_load.pop(0)
             dest = raw_pool.tile([P, LOAD], BF16, name="raw", tag="raw")
-            if kind == "proj":
+            if kind == "proj" and idx == 0 and HEAD == 1:
+                for half in range(2):
+                    nc.sync.dma_start(out=dest[:, LOAD // 2 * half:LOAD // 2 * (half + 1)].rearrange("p (a f) -> p a f", a=2),
+                                      in_=proj_rows[:, 2 * half:2 * half + 2, :])
+            elif kind == "proj":
                 nc.sync.dma_start(out=dest[:].rearrange("p (a f) -> p a f", a=4), in_=proj_rows[:, 4 * idx:4 * idx + 4, :])
             elif kind == "x":
                 nc.sync.dma_start(out=dest[:].rearrange("p (i k) -> p i k", i=2), in_=x_rows[:, 2 * idx:2 * idx + 2, :])
@@ -191,6 +198,9 @@ def tile_adaptiveinputsoftmax_pa_kernel(tc, x, tail_proj_0, tail_w_0, cluster_pr
 
         spread = {}
 
+        def copy_on_gpsimd(out, in_):
+            nc.gpsimd.tensor_scalar(out=out, in0=in_, scalar1=1.0, scalar2=0.0, op0=ALU.mult, op1=ALU.add)
+
         def spread_w(c, which):
             by_column = raw[("w", c)][:].rearrange("p (t n) -> p n t", t=PACK)
             for first in [WORDS - TENSOR_COLS[c] + SPREAD_BANK_COLS * which]:
@@ -208,10 +218,15 @@ def tile_adaptiveinputsoftmax_pa_kernel(tc, x, tail_proj_0, tail_w_0, cluster_pr
             new_grouped("w", c)
             regroup(nc.vector.tensor_copy, grouped[("w", c)][:], raw[("w", c)][:], 0, W_VECTOR_COLS[c])
             one_small_operation()
+            if W_GPSIMD_COLS[c]:
+                cols = slice(W_VECTOR_COLS[c] - OVERLAP, W_VECTOR_COLS[c] + W_GPSIMD_COLS[c])
+                copy_on_gpsimd(out=grouped[("w", c)][:].rearrange("p (n t) -> p n t", t=PACK)[:, cols, :],
+                               in_=raw[("w", c)][:].rearrange("p (t n) -> p n t", t=PACK)[:, cols, :])
             for first, bank in spread.get(c, []):
                 cols = min(SPREAD_BANK_COLS, WORDS - first)
                 nc.scalar.copy(out=grouped[("w", c)][:, PACK * first:PACK * (first + cols)], in_=bank[:, 0:PACK * cols])
-            regroup(nc.scalar.copy, grouped[("w", c)][:], raw[("w", c)][:], W_VECTOR_COLS[c], WORDS - TENSOR_COLS[c])
+            regroup(nc.scalar.copy, grouped[("w", c)][:], raw[("w", c)][:], W_VECTOR_COLS[c] + W_GPSIMD_COLS[c],
+                    WORDS - TENSOR_COLS[c])
 
         rows = {}
         exp_ready = []
@@ -330,15 +345,26 @@ def tile_adaptiveinputsoftmax_pa_kernel(tc, x, tail_proj_0, tail_w_0, cluster_pr
 
         for ahead in range(LOADS_AHEAD):
             load_next()
-        transpose_x(0)
-        copy_x(0)
-        load_next()
-        regroup_proj(0)
-        load_next()
-        quantise("x", 0)
-        regroup_proj(1)
-        load_next()
-        quantise("proj", 0)
+        if HEAD == 1:
+            regroup_proj(0)
+            load_next()
+            transpose_x(0)
+            copy_x(0)
+            load_next()
+            quantise("proj", 0)
+            regroup_proj(1)
+            load_next()
+            quantise("x", 0)
+        else:
+            transpose_x(0)
+            copy_x(0)
+            load_next()
+            regroup_proj(0)
+            load_next()
+            quantise("x", 0)
+            regroup_proj(1)
+            load_next()
+            quantise("proj", 0)
         transpose_x(1)
         quantise("proj", 1)
         multiply_h(0)

@@ -25,9 +25,9 @@ PASS_PAIRS = P * PACK // 2
 TILES = TOKENS // P
 BANK = 512
 BANKS = V0 // BANK
-GROUP_BANKS = [4, 4, 4, 4]
-MOST_GROUPS = BANKS // min(GROUP_BANKS)
-WIDEST_GROUP = max(GROUP_BANKS) * BANK
+GROUP_BANKS = 4
+GROUP = GROUP_BANKS * BANK
+GROUPS = V0 // GROUP
 LOAD = 4096
 WORDS = LOAD // PACK
 LOAD_TOKENS = LOAD // H * P
@@ -37,18 +37,12 @@ RUN = 4
 
 LOADS_AHEAD = 5
 PROJ_VECTOR_COLS = 256
-W_VECTOR_COLS = [576, 576, 320, 320, 320, 320, 320, 320]
-TENSOR_COLS = [0, 0, 0, 0, 0, 0, 0, 0]
-SPREAD_COLS = 128
-SPREAD_BANK_COLS = 256
-W_GPSIMD_COLS = [0, 0, 160, 160, 160, 160, 160, 160]
+W_VECTOR_COLS = [576, 576] + [320] * (CHUNKS - 2)
+W_GPSIMD_COLS = [0, 0] + [224] * (CHUNKS - 2)
 X_VECTOR_BANKS = 1
-LOGITS_LAG = 1
-OVERLAP = 0
-HEAD = 0
-H_STEP = 0
+MAX_LAG = 2
 TOTAL_BEHIND_BANK = [0, 1, 1]
-GPSIMD_GROUPS = [BANKS // GROUP_BANKS[0], 4, 2]
+GPSIMD_GROUPS = [4, 4, 2]
 
 
 def regroup(copy, dst, src, first, last):
@@ -70,16 +64,13 @@ def tile_adaptiveinputsoftmax_pa_kernel(tc, x, tail_proj_0, tail_w_0, cluster_pr
         raw_pool = ctx.enter_context(tc.tile_pool(name="raw", bufs=LOADS_AHEAD))
         grouped_pool = ctx.enter_context(tc.tile_pool(name="grouped", bufs=3))
         h_pool = ctx.enter_context(tc.tile_pool(name="h", bufs=2))
-        numerator_pool = ctx.enter_context(tc.tile_pool(name="numerators", bufs=12))
+        numerator_pool = ctx.enter_context(tc.tile_pool(name="numerators", bufs=3 * GROUPS))
         row_pool = ctx.enter_context(tc.tile_pool(name="row", bufs=TILES))
-        psum = ctx.enter_context(tc.psum_pool(name="psum", bufs=6))
-        psum_spread = ctx.enter_context(tc.psum_pool(name="psum_spread", bufs=2))
+        psum = ctx.enter_context(tc.psum_pool(name="psum", bufs=8))
         ctx.enter_context(tc.manual_schedule())
 
         identity = keep.tile([P, P], F32, name="identity")
         make_identity(nc, identity[:])
-        identity_bf16 = keep.tile([P, P], BF16, name="identity_bf16")
-        make_identity(nc, identity_bf16[:])
         zero = keep.tile([P, 1], F32, name="zero")
         nc.vector.memset(zero[:], 0.0)
         one = keep.tile([P, 1], F32, name="one")
@@ -97,7 +88,7 @@ def tile_adaptiveinputsoftmax_pa_kernel(tc, x, tail_proj_0, tail_w_0, cluster_pr
         prob_bf16 = keep.tile([P, TILES], BF16, name="prob_bf16")
         prob = keep.tile([P, TILES], F32, name="prob")
 
-        to_load = ([("proj", 0), ("x", 0), ("proj", 1), ("x", 1)] if HEAD == 1 else [("x", 0), ("proj", 0), ("proj", 1), ("x", 1)]) + [("w", c) for c in range(CHUNKS)]
+        to_load = [("x", 0), ("proj", 0), ("proj", 1), ("x", 1)] + [("w", c) for c in range(CHUNKS)]
         raw = {}
         grouped = {}
 
@@ -106,11 +97,7 @@ def tile_adaptiveinputsoftmax_pa_kernel(tc, x, tail_proj_0, tail_w_0, cluster_pr
                 return
             kind, idx = to_load.pop(0)
             dest = raw_pool.tile([P, LOAD], BF16, name="raw", tag="raw")
-            if kind == "proj" and idx == 0 and HEAD == 1:
-                for half in range(2):
-                    nc.sync.dma_start(out=dest[:, LOAD // 2 * half:LOAD // 2 * (half + 1)].rearrange("p (a f) -> p a f", a=2),
-                                      in_=proj_rows[:, 2 * half:2 * half + 2, :])
-            elif kind == "proj":
+            if kind == "proj":
                 nc.sync.dma_start(out=dest[:].rearrange("p (a f) -> p a f", a=4), in_=proj_rows[:, 4 * idx:4 * idx + 4, :])
             elif kind == "x":
                 nc.sync.dma_start(out=dest[:].rearrange("p (i k) -> p i k", i=2), in_=x_rows[:, 2 * idx:2 * idx + 2, :])
@@ -125,7 +112,7 @@ def tile_adaptiveinputsoftmax_pa_kernel(tc, x, tail_proj_0, tail_w_0, cluster_pr
         soon = []
         later = []
 
-        def one_small_operation():
+        def small_operations():
             if soon:
                 soon.pop(0)()
             if later:
@@ -135,7 +122,7 @@ def tile_adaptiveinputsoftmax_pa_kernel(tc, x, tail_proj_0, tail_w_0, cluster_pr
             words, scales = operands[kind]
             cols = slice(WORDS * idx, WORDS * (idx + 1))
             nc.vector.quantize_mx(out=words[:, cols].bitcast(FP8X4), scales=scales[:, cols], in_=grouped[(kind, idx)][:])
-            one_small_operation()
+            small_operations()
 
         x_banks = {}
 
@@ -171,10 +158,7 @@ def tile_adaptiveinputsoftmax_pa_kernel(tc, x, tail_proj_0, tail_w_0, cluster_pr
         h_grouped = {}
 
         def multiply_h(tile):
-            if tile < 2 or H_STEP == 0:
-                bank = psum.tile([P, BANK], F32, name="bank", tag="bank")
-            else:
-                bank = psum_spread.tile([P, BANK], F32, name="spread", tag="spread")
+            bank = psum.tile([P, BANK], F32, name="bank", tag="bank")
             for t in range(PACK):
                 for j in range(PASSES):
                     proj_cols = slice(P0 * j + P * t, P0 * j + P * (t + 1))
@@ -196,47 +180,24 @@ def tile_adaptiveinputsoftmax_pa_kernel(tc, x, tail_proj_0, tail_w_0, cluster_pr
             nc.vector.quantize_mx(out=h_words[:, tokens].bitcast(FP8X4), scales=h_scales[:, tokens],
                                   in_=h_grouped[tile][:])
 
-        spread = {}
-
-        def copy_on_gpsimd(out, in_):
-            nc.gpsimd.tensor_scalar(out=out, in0=in_, scalar1=1.0, scalar2=0.0, op0=ALU.mult, op1=ALU.add)
-
-        def spread_w(c, which):
-            by_column = raw[("w", c)][:].rearrange("p (t n) -> p n t", t=PACK)
-            for first in [WORDS - TENSOR_COLS[c] + SPREAD_BANK_COLS * which]:
-                if first >= WORDS:
-                    continue
-                bank = psum_spread.tile([P, PACK * SPREAD_BANK_COLS], BF16, name="spread", tag="spread")
-                for part in range(min(SPREAD_BANK_COLS, WORDS - first) // SPREAD_COLS):
-                    cols = slice(first + SPREAD_COLS * part, first + SPREAD_COLS * (part + 1))
-                    side_by_side = bank[:, PACK * SPREAD_COLS * part:PACK * SPREAD_COLS * (part + 1)]
-                    nc.tensor.matmul(out=side_by_side.rearrange("p (n t) -> p n t", t=PACK), lhsT=identity_bf16[:],
-                                     rhs=by_column[:, cols, :], start=True, stop=True)
-                spread.setdefault(c, []).append((first, bank))
-
         def regroup_w(c):
             new_grouped("w", c)
-            regroup(nc.vector.tensor_copy, grouped[("w", c)][:], raw[("w", c)][:], 0, W_VECTOR_COLS[c])
-            one_small_operation()
+            dst, src = grouped[("w", c)][:], raw[("w", c)][:]
+            regroup(nc.vector.tensor_copy, dst, src, 0, W_VECTOR_COLS[c])
+            small_operations()
             if W_GPSIMD_COLS[c]:
-                cols = slice(W_VECTOR_COLS[c] - OVERLAP, W_VECTOR_COLS[c] + W_GPSIMD_COLS[c])
-                copy_on_gpsimd(out=grouped[("w", c)][:].rearrange("p (n t) -> p n t", t=PACK)[:, cols, :],
-                               in_=raw[("w", c)][:].rearrange("p (t n) -> p n t", t=PACK)[:, cols, :])
-            for first, bank in spread.get(c, []):
-                cols = min(SPREAD_BANK_COLS, WORDS - first)
-                nc.scalar.copy(out=grouped[("w", c)][:, PACK * first:PACK * (first + cols)], in_=bank[:, 0:PACK * cols])
-            regroup(nc.scalar.copy, grouped[("w", c)][:], raw[("w", c)][:], W_VECTOR_COLS[c] + W_GPSIMD_COLS[c],
-                    WORDS - TENSOR_COLS[c])
+                cols = slice(W_VECTOR_COLS[c], W_VECTOR_COLS[c] + W_GPSIMD_COLS[c])
+                nc.gpsimd.tensor_scalar(out=dst.rearrange("p (n t) -> p n t", t=PACK)[:, cols, :],
+                                        in0=src.rearrange("p (t n) -> p n t", t=PACK)[:, cols, :],
+                                        scalar1=1.0, scalar2=0.0, op0=ALU.mult, op1=ALU.add)
+            regroup(nc.scalar.copy, dst, src, W_VECTOR_COLS[c] + W_GPSIMD_COLS[c], WORDS)
 
         rows = {}
         exp_ready = []
 
-        def groups_of(tile):
-            return BANKS // GROUP_BANKS[tile]
-
         def start_tile(tile):
             rows[tile] = {
-                "shift": row_pool.tile([P, MOST_GROUPS], F32, name="shift", tag="shift"),
+                "shift": row_pool.tile([P, GROUPS], F32, name="shift", tag="shift"),
                 "sums": row_pool.tile([P, BANKS], F32, name="sums", tag="sums"),
                 "maxima": row_pool.tile([P, BANKS], F32, name="maxima", tag="maxima"),
                 "numerators": {}, "bank": {},
@@ -245,10 +206,7 @@ def tile_adaptiveinputsoftmax_pa_kernel(tc, x, tail_proj_0, tail_w_0, cluster_pr
         def multiply_logits(tile, b):
             tokens = slice(P * tile, P * (tile + 1))
             cols = slice(BANK * b, BANK * (b + 1))
-            if (tile > 0 or sum(TENSOR_COLS) == 0) and b % 4 == 0:
-                bank = psum_spread.tile([P, BANK], F32, name="spread", tag="spread")
-            else:
-                bank = psum.tile([P, BANK], F32, name="bank", tag="bank")
+            bank = psum.tile([P, BANK], F32, name="bank", tag="bank")
             nc.tensor.matmul_mx(out=bank[:], lhsT=h_words[:, tokens].bitcast(FP8X4), lhsT_scale=h_scales[:, tokens],
                                 rhs=w_words[:, cols].bitcast(FP8X4), rhs_scale=w_scales[:, cols], start=True, stop=True)
             rows[tile]["bank"][b] = bank
@@ -257,79 +215,73 @@ def tile_adaptiveinputsoftmax_pa_kernel(tc, x, tail_proj_0, tail_w_0, cluster_pr
             for ready in range(min(count, len(exp_ready))):
                 tile, b = exp_ready.pop(0)
                 row = rows[tile]
-                g, place = divmod(b, GROUP_BANKS[tile])
+                g, place = divmod(b, GROUP_BANKS)
                 if place == 0:
-                    row["numerators"][g] = numerator_pool.tile([P, BANK * GROUP_BANKS[tile]], F32, name="numerators",
-                                                               tag="numerators")
+                    row["numerators"][g] = numerator_pool.tile([P, GROUP], F32, name="numerators", tag="numerators")
                 nc.scalar.activation(out=row["numerators"][g][:, BANK * place:BANK * (place + 1)], in_=row["bank"][b][:],
                                      func=AF.Exp, bias=row["shift"][:, g:g + 1], scale=1.0,
                                      accum_out=row["sums"][:, b:b + 1])
 
         def group_shift(tile, g, at_once):
             row = rows[tile]
-            count = groups_of(tile)
-            nc.vector.tensor_reduce(out=row["shift"][:, g:g + 1], in_=row["maxima"][:, 0:GROUP_BANKS[tile] * (g + 1)],
-                                    axis=AX.X, op=ALU.max, negate=True)
-            exp_ready.extend([(tile, b) for b in range(GROUP_BANKS[tile] * g, GROUP_BANKS[tile] * (g + 1))])
-            if g == count - 1:
-                row["f"] = row_pool.tile([P, MOST_GROUPS], F32, name="f", tag="f")
-                nc.scalar.activation(out=row["f"][:, 0:count], in_=row["shift"][:, 0:count], func=AF.Exp,
-                                     bias=row["shift"][:, count - 1:count], scale=-1.0)
+            nc.vector.tensor_reduce(out=row["shift"][:, g:g + 1], in_=row["maxima"][:, 0:GROUP_BANKS * (g + 1)], axis=AX.X,
+                                    op=ALU.max, negate=True)
+            exp_ready.extend([(tile, b) for b in range(GROUP_BANKS * g, GROUP_BANKS * (g + 1))])
+            if g == GROUPS - 1:
+                row["f"] = row_pool.tile([P, GROUPS], F32, name="f", tag="f")
+                nc.scalar.activation(out=row["f"][:], in_=row["shift"][:], func=AF.Exp,
+                                     bias=row["shift"][:, GROUPS - 1:GROUPS], scale=-1.0)
             if at_once:
-                exponentials(GROUP_BANKS[tile])
+                exponentials(GROUP_BANKS)
 
         def bank_maximum(tile, b, at_once):
             row = rows[tile]
-            g, place = divmod(b, GROUP_BANKS[tile])
             nc.vector.tensor_reduce(out=row["maxima"][:, b:b + 1], in_=row["bank"][b][:], axis=AX.X, op=ALU.max)
-            one_small_operation()
-            if place == GROUP_BANKS[tile] - 1:
-                soon.append(lambda: group_shift(tile, g, at_once))
+            small_operations()
+            if b % GROUP_BANKS == GROUP_BANKS - 1:
+                soon.append(lambda: group_shift(tile, b // GROUP_BANKS, at_once))
 
-        def total_steps(tile, engine, then, at_a_stroke=False):
+        def total_steps(tile, engine, then, gpsimd_idle):
             row = rows[tile]
-            width = GROUP_BANKS[tile]
-            products = row_pool.tile([P, max(GROUP_BANKS)], F32, name="products", tag="products")
-            total = row_pool.tile([P, MOST_GROUPS], F32, name="total", tag="total")
+            products = row_pool.tile([P, GROUP_BANKS], F32, name="products", tag="products")
+            total = row_pool.tile([P, GROUPS], F32, name="total", tag="total")
             inverse = row_pool.tile([P, 1], F32, name="inverse", tag="inverse")
-            row["factor"] = row_pool.tile([P, MOST_GROUPS], F32, name="factor", tag="factor")
-
-            count = groups_of(tile)
+            row["factor"] = row_pool.tile([P, GROUPS], F32, name="factor", tag="factor")
 
             def add_group(g):
-                nc.vector.tensor_scalar(out=products[:, 0:width], in0=row["sums"][:, width * g:width * (g + 1)],
+                nc.vector.tensor_scalar(out=products[:], in0=row["sums"][:, GROUP_BANKS * g:GROUP_BANKS * (g + 1)],
                                         scalar1=row["f"][:, g:g + 1], scalar2=(total[:, g - 1:g] if g else 0.0),
                                         op0=ALU.mult, op1=ALU.add, accum_out=total[:, g:g + 1])
 
             def group_sums():
-                nc.vector.tensor_reduce(out=sums_by_group[:, 0:count - 1],
-                                        in_=row["sums"][:, 0:width * (count - 1)].rearrange("p (g b) -> p g b", b=width),
+                nc.vector.tensor_reduce(out=sums_by_group[:, 0:GROUPS - 1],
+                                        in_=row["sums"][:, 0:GROUP_BANKS * (GROUPS - 1)].rearrange("p (g b) -> p g b",
+                                                                                                  b=GROUP_BANKS),
                                         axis=AX.X, op=ALU.add)
 
             def weigh_groups():
-                nc.vector.scalar_tensor_tensor(out=weighted[:, 0:count - 1], in0=sums_by_group[:, 0:count - 1], scalar=1.0,
-                                               in1=row["f"][:, 0:count - 1], op0=ALU.mult, op1=ALU.mult,
-                                               accum_out=total[:, count - 2:count - 1])
+                nc.vector.scalar_tensor_tensor(out=weighted[:, 0:GROUPS - 1], in0=sums_by_group[:, 0:GROUPS - 1], scalar=1.0,
+                                               in1=row["f"][:, 0:GROUPS - 1], op0=ALU.mult, op1=ALU.mult,
+                                               accum_out=total[:, GROUPS - 2:GROUPS - 1])
 
             def factors():
-                nc.vector.reciprocal(out=inverse[:], in_=total[:, count - 1:count])
-                engine.tensor_scalar(out=row["factor"][:, 0:count], in0=row["f"][:, 0:count],
-                                     scalar1=inverse[:], scalar2=prob[:, tile:tile + 1], op0=ALU.mult, op1=ALU.mult)
+                nc.vector.reciprocal(out=inverse[:], in_=total[:, GROUPS - 1:GROUPS])
+                engine.tensor_scalar(out=row["factor"][:], in0=row["f"][:], scalar1=inverse[:],
+                                     scalar2=prob[:, tile:tile + 1], op0=ALU.mult, op1=ALU.mult)
                 then()
 
             def adder(g):
                 return lambda: add_group(g)
 
-            if at_a_stroke:
-                sums_by_group = row_pool.tile([P, MOST_GROUPS], F32, name="sums_by_group", tag="sums_by_group")
-                weighted = row_pool.tile([P, MOST_GROUPS], F32, name="weighted", tag="weighted")
-                return [group_sums, weigh_groups, adder(count - 1), factors]
-            return [adder(g) for g in range(count)] + [factors]
+            if gpsimd_idle:
+                sums_by_group = row_pool.tile([P, GROUPS], F32, name="sums_by_group", tag="sums_by_group")
+                weighted = row_pool.tile([P, GROUPS], F32, name="weighted", tag="weighted")
+                return [group_sums, weigh_groups, adder(GROUPS - 1), factors]
+            return [adder(g) for g in range(GROUPS)] + [factors]
 
         def scale_and_store(tile, g, engine):
             numerators = rows[tile]["numerators"][g][:]
             factor = rows[tile]["factor"][:, g:g + 1]
-            width = BANK * GROUP_BANKS[tile]
             if engine == "gpsimd":
                 nc.gpsimd.tensor_scalar(out=numerators, in0=numerators, scalar1=factor, scalar2=0.0,
                                         op0=ALU.mult, op1=ALU.add)
@@ -337,7 +289,7 @@ def tile_adaptiveinputsoftmax_pa_kernel(tc, x, tail_proj_0, tail_w_0, cluster_pr
                 nc.vector.tensor_scalar(out=numerators, in0=numerators, scalar1=factor, scalar2=None, op0=ALU.mult)
             else:
                 nc.scalar.activation(out=numerators, in_=numerators, func=AF.Copy, scale=factor)
-            nc.sync.dma_start(out=out_rows[P * tile:P * (tile + 1), width * g:width * (g + 1)], in_=numerators)
+            nc.sync.dma_start(out=out_rows[P * tile:P * (tile + 1), GROUP * g:GROUP * (g + 1)], in_=numerators)
 
         def gpsimd_share(tile):
             for g in range(GPSIMD_GROUPS[tile]):
@@ -345,26 +297,15 @@ def tile_adaptiveinputsoftmax_pa_kernel(tc, x, tail_proj_0, tail_w_0, cluster_pr
 
         for ahead in range(LOADS_AHEAD):
             load_next()
-        if HEAD == 1:
-            regroup_proj(0)
-            load_next()
-            transpose_x(0)
-            copy_x(0)
-            load_next()
-            quantise("proj", 0)
-            regroup_proj(1)
-            load_next()
-            quantise("x", 0)
-        else:
-            transpose_x(0)
-            copy_x(0)
-            load_next()
-            regroup_proj(0)
-            load_next()
-            quantise("x", 0)
-            regroup_proj(1)
-            load_next()
-            quantise("proj", 0)
+        transpose_x(0)
+        copy_x(0)
+        load_next()
+        regroup_proj(0)
+        load_next()
+        quantise("x", 0)
+        regroup_proj(1)
+        load_next()
+        quantise("proj", 0)
         transpose_x(1)
         quantise("proj", 1)
         multiply_h(0)
@@ -373,34 +314,27 @@ def tile_adaptiveinputsoftmax_pa_kernel(tc, x, tail_proj_0, tail_w_0, cluster_pr
         load_next()
 
         start_tile(0)
-        for c in range(CHUNKS + LOGITS_LAG + 1):
+        for c in range(CHUNKS + MAX_LAG):
             if 1 <= c <= CHUNKS:
                 quantise("w", c - 1)
             if c < CHUNKS:
                 regroup_w(c)
                 load_next()
-            if c + 1 < CHUNKS:
-                spread_w(c + 1, 0)
-            if 0 <= c - LOGITS_LAG < CHUNKS:
-                for b in range(CHUNK_BANKS * (c - LOGITS_LAG), CHUNK_BANKS * (c - LOGITS_LAG + 1)):
+            if 1 <= c <= CHUNKS:
+                for b in range(CHUNK_BANKS * (c - 1), CHUNK_BANKS * c):
                     multiply_logits(0, b)
-            if c + 1 < CHUNKS:
-                spread_w(c + 1, 1)
             if c == 0:
                 quantise("x", 1)
                 copy_h(0)
                 copy_h(1)
-            if c == H_STEP:
                 multiply_h(2)
                 multiply_h(3)
-            if c == 0:
                 quantise_h(0)
-            if c == H_STEP + 1:
+            if c == 1:
                 copy_h(2)
                 copy_h(3)
-            if c == 1:
                 quantise_h(1)
-            if c == H_STEP + 2:
+            if c == 2:
                 quantise_h(2)
                 quantise_h(3)
             if c == CHUNKS - 1:
@@ -409,28 +343,28 @@ def tile_adaptiveinputsoftmax_pa_kernel(tc, x, tail_proj_0, tail_w_0, cluster_pr
             if c == CHUNKS + 1:
                 nc.vector.tensor_copy(out=prob[:], in_=prob_bf16[:])
             exponentials(CHUNK_BANKS)
-            if c >= LOGITS_LAG + 1:
-                for b in range(CHUNK_BANKS * (c - LOGITS_LAG - 1), CHUNK_BANKS * (c - LOGITS_LAG)):
+            if c >= MAX_LAG:
+                for b in range(CHUNK_BANKS * (c - MAX_LAG), CHUNK_BANKS * (c - MAX_LAG + 1)):
                     bank_maximum(0, b, c >= CHUNKS)
 
         for tile in range(1, TILES):
             start_tile(tile)
             for b in range(BANKS):
-                if b % GROUP_BANKS[tile] == 0:
-                    for ahead in range(GROUP_BANKS[tile]):
+                if b % GROUP_BANKS == 0:
+                    for ahead in range(GROUP_BANKS):
                         multiply_logits(tile, b + ahead)
                 bank_maximum(tile, b, True)
                 if b == TOTAL_BEHIND_BANK[tile - 1]:
                     later.extend(total_steps(tile - 1, nc.gpsimd, lambda: gpsimd_share(tile - 1), tile == 1))
         while soon or later:
-            one_small_operation()
+            small_operations()
 
-        for g in range(GPSIMD_GROUPS[TILES - 2], groups_of(TILES - 2)):
+        for g in range(GPSIMD_GROUPS[TILES - 2], GROUPS):
             scale_and_store(TILES - 2, g, "vector")
 
         def last_tile():
             for g, engine in enumerate(["vector", "scalar", "vector", "vector"]):
                 scale_and_store(TILES - 1, g, engine)
 
-        for operation in total_steps(TILES - 1, nc.vector, last_tile):
+        for operation in total_steps(TILES - 1, nc.vector, last_tile, False):
             operation()

from contextlib import ExitStack

import concourse.mybir as mybir
from concourse.masks import make_identity

F32 = mybir.dt.float32
BF16 = mybir.dt.bfloat16
U32 = mybir.dt.uint32
U8 = mybir.dt.uint8
FP8X4 = mybir.dt.float8_e4m3fn_x4
AF = mybir.ActivationFunctionType
ALU = mybir.AluOpType
AX = mybir.AxisListType

P = 128
TOKENS = 512
H = 2048
P0 = 512
V0 = 8192
FLOPS = 2 * TOKENS * H * P0 + 2 * TOKENS * P0 * V0

PACK = 4
PASSES = H // (P * PACK)
PASS_PAIRS = P * PACK // 2
TILES = TOKENS // P
BANK = 512
BANKS = V0 // BANK
GROUP_BANKS = 4
GROUP = GROUP_BANKS * BANK
GROUPS = V0 // GROUP
LOAD = 4096
WORDS = LOAD // PACK
LOAD_TOKENS = LOAD // H * P
CHUNKS = P0 * V0 // (P * LOAD)
CHUNK_BANKS = WORDS // BANK
RUN = 4

LOADS_AHEAD = 5
PROJ_VECTOR_COLS = 256
W_VECTOR_COLS = [576, 576] + [320] * (CHUNKS - 2)
W_GPSIMD_COLS = [0, 0] + [224] * (CHUNKS - 2)
X_VECTOR_BANKS = 1
MAX_LAG = 2
TOTAL_BEHIND_BANK = [0, 1, 1]
GPSIMD_GROUPS = [4, 4, 2]


def regroup(copy, dst, src, first, last):
    d = dst.rearrange("p (c i t) -> p c t i", i=RUN, t=PACK)[:, first // RUN:last // RUN, :, :]
    s = src.rearrange("p (t c i) -> p c t i", t=PACK, i=RUN)[:, first // RUN:last // RUN, :, :]
    copy(out=d, in_=s)


def tile_adaptiveinputsoftmax_pa_kernel(tc, x, tail_proj_0, tail_w_0, cluster_prob, out):
    nc = tc.nc
    x_rows = x.rearrange("n t h -> (n t) h").rearrange("(i p) k -> p i k", p=P)
    proj_rows = tail_proj_0.rearrange("(a p e) n -> p a (e n)", p=P, e=2)
    w_rows = tail_w_0.rearrange("(t p) n -> p t n", p=P)
    out_rows = out.rearrange("n t v -> (n t) v")
    prob_cols = cluster_prob.rearrange("n t o -> (n t o)").rearrange("(i p) -> p i", p=P)

    with ExitStack() as ctx:
        keep = ctx.enter_context(tc.tile_pool(name="keep", bufs=1))
        raw_pool = ctx.enter_context(tc.tile_pool(name="raw", bufs=LOADS_AHEAD))
        grouped_pool = ctx.enter_context(tc.tile_pool(name="grouped", bufs=3))
        h_pool = ctx.enter_context(tc.tile_pool(name="h", bufs=2))
        numerator_pool = ctx.enter_context(tc.tile_pool(name="numerators", bufs=3 * GROUPS))
        row_pool = ctx.enter_context(tc.tile_pool(name="row", bufs=TILES))
        psum = ctx.enter_context(tc.psum_pool(name="psum", bufs=8))
        ctx.enter_context(tc.manual_schedule())

        identity = keep.tile([P, P], F32, name="identity")
        make_identity(nc, identity[:])
        zero = keep.tile([P, 1], F32, name="zero")
        nc.vector.memset(zero[:], 0.0)
        one = keep.tile([P, 1], F32, name="one")
        nc.scalar.activation(out=one[:], in_=zero[:], func=AF.Exp)

        proj_words = keep.tile([P, PASSES * P0], U32, name="proj_words", align_bytes=64)
        proj_scales = keep.tile([P, PASSES * P0], U8, name="proj_scales", align_bytes=64)
        x_words = keep.tile([P, PASSES * TOKENS], U32, name="x_words", align_bytes=64)
        x_scales = keep.tile([P, PASSES * TOKENS], U8, name="x_scales", align_bytes=64)
        h_words = keep.tile([P, TOKENS], U32, name="h_words", align_bytes=64)
        h_scales = keep.tile([P, TOKENS], U8, name="h_scales", align_bytes=64)
        w_words = keep.tile([P, V0], U32, name="w_words", align_bytes=64)
        w_scales = keep.tile([P, V0], U8, name="w_scales", align_bytes=64)
        operands = {"proj": (proj_words, proj_scales), "x": (x_words, x_scales), "w": (w_words, w_scales)}
        prob_bf16 = keep.tile([P, TILES], BF16, name="prob_bf16")
        prob = keep.tile([P, TILES], F32, name="prob")

        to_load = [("x", 0), ("proj", 0), ("proj", 1), ("x", 1)] + [("w", c) for c in range(CHUNKS)]
        raw = {}
        grouped = {}

        def load_next():
            if not to_load:
                return
            kind, idx = to_load.pop(0)
            dest = raw_pool.tile([P, LOAD], BF16, name="raw", tag="raw")
            if kind == "proj":
                nc.sync.dma_start(out=dest[:].rearrange("p (a f) -> p a f", a=4), in_=proj_rows[:, 4 * idx:4 * idx + 4, :])
            elif kind == "x":
                nc.sync.dma_start(out=dest[:].rearrange("p (i k) -> p i k", i=2), in_=x_rows[:, 2 * idx:2 * idx + 2, :])
            else:
                nc.sync.dma_start(out=dest[:].rearrange("p (t n) -> p t n", t=PACK),
                                  in_=w_rows[:, :, WORDS * idx:WORDS * (idx + 1)])
            raw[(kind, idx)] = dest

        def new_grouped(kind, idx):
            grouped[(kind, idx)] = grouped_pool.tile([P, LOAD], BF16, name="grouped", tag="grouped", align_bytes=64)

        soon = []
        later = []

        def small_operations():
            if soon:
                soon.pop(0)()
            if later:
                later.pop(0)()

        def quantise(kind, idx):
            words, scales = operands[kind]
            cols = slice(WORDS * idx, WORDS * (idx + 1))
            nc.vector.quantize_mx(out=words[:, cols].bitcast(FP8X4), scales=scales[:, cols], in_=grouped[(kind, idx)][:])
            small_operations()

        x_banks = {}

        def transpose_x(idx):
            new_grouped("x", idx)
            pairs = raw[("x", idx)][:].bitcast(F32)
            x_banks[idx] = []
            for j in range(PASSES):
                bank = psum.tile([P, BANK], F32, name="bank", tag="bank")
                for u in range(2):
                    for i in range(2):
                        first = H // 2 * i + PASS_PAIRS * j + P * u
                        nc.tensor.transpose(out=bank[:, LOAD_TOKENS * u + P * i:LOAD_TOKENS * u + P * (i + 1)],
                                            in_=pairs[:, first:first + P], identity=identity[:])
                x_banks[idx].append(bank)

        def copy_x(idx):
            pairs = grouped[("x", idx)][:].bitcast(F32)
            for j in range(PASSES):
                copy = nc.vector.tensor_copy if j >= PASSES - X_VECTOR_BANKS else nc.scalar.copy
                copy(out=pairs[:, BANK * j:BANK * (j + 1)].rearrange("p (m u) -> p m u", u=2),
                     in_=x_banks[idx][j][:].rearrange("p (u m) -> p m u", u=2))

        def regroup_proj(idx):
            new_grouped("proj", idx)
            for half in range(2):
                part = slice(PACK * P0 * half, PACK * P0 * (half + 1))
                dst, src = grouped[("proj", idx)][:, part], raw[("proj", idx)][:, part]
                regroup(nc.vector.tensor_copy, dst, src, 0, PROJ_VECTOR_COLS)
                regroup(nc.scalar.copy, dst, src, PROJ_VECTOR_COLS, P0)

        h_bank = {}
        h_grouped = {}

        def multiply_h(tile):
            bank = psum.tile([P, BANK], F32, name="bank", tag="bank")
            for t in range(PACK):
                for j in range(PASSES):
                    proj_cols = slice(P0 * j + P * t, P0 * j + P * (t + 1))
                    first = WORDS * (tile // 2) + LOAD_TOKENS * j + P * (tile % 2)
                    tokens = slice(first, first + P)
                    nc.tensor.matmul_mx(out=bank[:, P * t:P * (t + 1)],
                                        lhsT=proj_words[:, proj_cols].bitcast(FP8X4), lhsT_scale=proj_scales[:, proj_cols],
                                        rhs=x_words[:, tokens].bitcast(FP8X4), rhs_scale=x_scales[:, tokens],
                                        start=(j == 0), stop=(j == PASSES - 1))
            h_bank[tile] = bank

        def copy_h(tile):
            h_grouped[tile] = h_pool.tile([P, PACK * P], BF16, name="h_grouped", tag="h_grouped", align_bytes=64)
            nc.scalar.copy(out=h_grouped[tile][:].rearrange("p (m t) -> p m t", t=PACK),
                           in_=h_bank[tile][:].rearrange("p (t m) -> p m t", t=PACK))

        def quantise_h(tile):
            tokens = slice(P * tile, P * (tile + 1))
            nc.vector.quantize_mx(out=h_words[:, tokens].bitcast(FP8X4), scales=h_scales[:, tokens],
                                  in_=h_grouped[tile][:])

        def regroup_w(c):
            new_grouped("w", c)
            dst, src = grouped[("w", c)][:], raw[("w", c)][:]
            regroup(nc.vector.tensor_copy, dst, src, 0, W_VECTOR_COLS[c])
            small_operations()
            if W_GPSIMD_COLS[c]:
                cols = slice(W_VECTOR_COLS[c], W_VECTOR_COLS[c] + W_GPSIMD_COLS[c])
                nc.gpsimd.tensor_scalar(out=dst.rearrange("p (n t) -> p n t", t=PACK)[:, cols, :],
                                        in0=src.rearrange("p (t n) -> p n t", t=PACK)[:, cols, :],
                                        scalar1=1.0, scalar2=0.0, op0=ALU.mult, op1=ALU.add)
            regroup(nc.scalar.copy, dst, src, W_VECTOR_COLS[c] + W_GPSIMD_COLS[c], WORDS)

        rows = {}
        exp_ready = []

        def start_tile(tile):
            rows[tile] = {
                "shift": row_pool.tile([P, GROUPS], F32, name="shift", tag="shift"),
                "sums": row_pool.tile([P, BANKS], F32, name="sums", tag="sums"),
                "maxima": row_pool.tile([P, BANKS], F32, name="maxima", tag="maxima"),
                "numerators": {}, "bank": {},
            }

        def multiply_logits(tile, b):
            tokens = slice(P * tile, P * (tile + 1))
            cols = slice(BANK * b, BANK * (b + 1))
            bank = psum.tile([P, BANK], F32, name="bank", tag="bank")
            nc.tensor.matmul_mx(out=bank[:], lhsT=h_words[:, tokens].bitcast(FP8X4), lhsT_scale=h_scales[:, tokens],
                                rhs=w_words[:, cols].bitcast(FP8X4), rhs_scale=w_scales[:, cols], start=True, stop=True)
            rows[tile]["bank"][b] = bank

        def exponentials(count):
            for ready in range(min(count, len(exp_ready))):
                tile, b = exp_ready.pop(0)
                row = rows[tile]
                g, place = divmod(b, GROUP_BANKS)
                if place == 0:
                    row["numerators"][g] = numerator_pool.tile([P, GROUP], F32, name="numerators", tag="numerators")
                nc.scalar.activation(out=row["numerators"][g][:, BANK * place:BANK * (place + 1)], in_=row["bank"][b][:],
                                     func=AF.Exp, bias=row["shift"][:, g:g + 1], scale=1.0,
                                     accum_out=row["sums"][:, b:b + 1])

        def group_shift(tile, g, at_once):
            row = rows[tile]
            nc.vector.tensor_reduce(out=row["shift"][:, g:g + 1], in_=row["maxima"][:, 0:GROUP_BANKS * (g + 1)], axis=AX.X,
                                    op=ALU.max, negate=True)
            exp_ready.extend([(tile, b) for b in range(GROUP_BANKS * g, GROUP_BANKS * (g + 1))])
            if g == GROUPS - 1:
                row["f"] = row_pool.tile([P, GROUPS], F32, name="f", tag="f")
                nc.scalar.activation(out=row["f"][:], in_=row["shift"][:], func=AF.Exp,
                                     bias=row["shift"][:, GROUPS - 1:GROUPS], scale=-1.0)
            if at_once:
                exponentials(GROUP_BANKS)

        def bank_maximum(tile, b, at_once):
            row = rows[tile]
            nc.vector.tensor_reduce(out=row["maxima"][:, b:b + 1], in_=row["bank"][b][:], axis=AX.X, op=ALU.max)
            small_operations()
            if b % GROUP_BANKS == GROUP_BANKS - 1:
                soon.append(lambda: group_shift(tile, b // GROUP_BANKS, at_once))

        def total_steps(tile, engine, then, gpsimd_idle):
            row = rows[tile]
            products = row_pool.tile([P, GROUP_BANKS], F32, name="products", tag="products")
            total = row_pool.tile([P, GROUPS], F32, name="total", tag="total")
            inverse = row_pool.tile([P, 1], F32, name="inverse", tag="inverse")
            row["factor"] = row_pool.tile([P, GROUPS], F32, name="factor", tag="factor")

            def add_group(g):
                nc.vector.tensor_scalar(out=products[:], in0=row["sums"][:, GROUP_BANKS * g:GROUP_BANKS * (g + 1)],
                                        scalar1=row["f"][:, g:g + 1], scalar2=(total[:, g - 1:g] if g else 0.0),
                                        op0=ALU.mult, op1=ALU.add, accum_out=total[:, g:g + 1])

            def group_sums():
                nc.vector.tensor_reduce(out=sums_by_group[:, 0:GROUPS - 1],
                                        in_=row["sums"][:, 0:GROUP_BANKS * (GROUPS - 1)].rearrange("p (g b) -> p g b",
                                                                                                  b=GROUP_BANKS),
                                        axis=AX.X, op=ALU.add)

            def weigh_groups():
                nc.vector.scalar_tensor_tensor(out=weighted[:, 0:GROUPS - 1], in0=sums_by_group[:, 0:GROUPS - 1], scalar=1.0,
                                               in1=row["f"][:, 0:GROUPS - 1], op0=ALU.mult, op1=ALU.mult,
                                               accum_out=total[:, GROUPS - 2:GROUPS - 1])

            def factors():
                nc.vector.reciprocal(out=inverse[:], in_=total[:, GROUPS - 1:GROUPS])
                engine.tensor_scalar(out=row["factor"][:], in0=row["f"][:], scalar1=inverse[:],
                                     scalar2=prob[:, tile:tile + 1], op0=ALU.mult, op1=ALU.mult)
                then()

            def adder(g):
                return lambda: add_group(g)

            if gpsimd_idle:
                sums_by_group = row_pool.tile([P, GROUPS], F32, name="sums_by_group", tag="sums_by_group")
                weighted = row_pool.tile([P, GROUPS], F32, name="weighted", tag="weighted")
                return [group_sums, weigh_groups, adder(GROUPS - 1), factors]
            return [adder(g) for g in range(GROUPS)] + [factors]

        def scale_and_store(tile, g, engine):
            numerators = rows[tile]["numerators"][g][:]
            factor = rows[tile]["factor"][:, g:g + 1]
            if engine == "gpsimd":
                nc.gpsimd.tensor_scalar(out=numerators, in0=numerators, scalar1=factor, scalar2=0.0,
                                        op0=ALU.mult, op1=ALU.add)
            elif engine == "vector":
                nc.vector.tensor_scalar(out=numerators, in0=numerators, scalar1=factor, scalar2=None, op0=ALU.mult)
            else:
                nc.scalar.activation(out=numerators, in_=numerators, func=AF.Copy, scale=factor)
            nc.sync.dma_start(out=out_rows[P * tile:P * (tile + 1), GROUP * g:GROUP * (g + 1)], in_=numerators)

        def gpsimd_share(tile):
            for g in range(GPSIMD_GROUPS[tile]):
                scale_and_store(tile, g, "gpsimd")

        for ahead in range(LOADS_AHEAD):
            load_next()
        transpose_x(0)
        copy_x(0)
        load_next()
        regroup_proj(0)
        load_next()
        quantise("x", 0)
        regroup_proj(1)
        load_next()
        quantise("proj", 0)
        transpose_x(1)
        quantise("proj", 1)
        multiply_h(0)
        multiply_h(1)
        copy_x(1)
        load_next()

        start_tile(0)
        for c in range(CHUNKS + MAX_LAG):
            if 1 <= c <= CHUNKS:
                quantise("w", c - 1)
            if c < CHUNKS:
                regroup_w(c)
                load_next()
            if 1 <= c <= CHUNKS:
                for b in range(CHUNK_BANKS * (c - 1), CHUNK_BANKS * c):
                    multiply_logits(0, b)
            if c == 0:
                quantise("x", 1)
                copy_h(0)
                copy_h(1)
                multiply_h(2)
                multiply_h(3)
                quantise_h(0)
            if c == 1:
                copy_h(2)
                copy_h(3)
                quantise_h(1)
            if c == 2:
                quantise_h(2)
                quantise_h(3)
            if c == CHUNKS - 1:
                with nc.allow_non_contiguous_dma(reason="512 two-byte values, one column for each token tile"):
                    nc.sync.dma_start(out=prob_bf16[:], in_=prob_cols)
            if c == CHUNKS + 1:
                nc.vector.tensor_copy(out=prob[:], in_=prob_bf16[:])
            exponentials(CHUNK_BANKS)
            if c >= MAX_LAG:
                for b in range(CHUNK_BANKS * (c - MAX_LAG), CHUNK_BANKS * (c - MAX_LAG + 1)):
                    bank_maximum(0, b, c >= CHUNKS)

        for tile in range(1, TILES):
            start_tile(tile)
            for b in range(BANKS):
                if b % GROUP_BANKS == 0:
                    for ahead in range(GROUP_BANKS):
                        multiply_logits(tile, b + ahead)
                bank_maximum(tile, b, True)
                if b == TOTAL_BEHIND_BANK[tile - 1]:
                    later.extend(total_steps(tile - 1, nc.gpsimd, lambda: gpsimd_share(tile - 1), tile == 1))
        while soon or later:
            small_operations()

        for g in range(GPSIMD_GROUPS[TILES - 2], GROUPS):
            scale_and_store(TILES - 2, g, "vector")

        def last_tile():
            for g, engine in enumerate(["vector", "scalar", "vector", "vector"]):
                scale_and_store(TILES - 1, g, engine)

        for operation in total_steps(TILES - 1, nc.vector, last_tile, False):
            operation()
